import numpy as np
import ml_dtypes


def mxq(x, axis, fmt="e4m3"):
    dtype, down = {"e4m3": (ml_dtypes.float8_e4m3fn, 7), "e5m2": (ml_dtypes.float8_e5m2, 14)}[fmt]
    v = np.moveaxis(np.asarray(x, np.float32).astype(ml_dtypes.bfloat16).astype(np.float64), axis, -1)
    blocks = v.reshape(v.shape[:-1] + (-1, 32))
    amax = np.abs(blocks).max(-1, keepdims=True)
    byte = np.maximum(np.where(amax > 0, np.frexp(amax)[1] - 1 + 127, 0) - down, 1)
    scale = np.exp2(byte - 127.0)
    codes = (blocks / scale).astype(np.float32).astype(dtype).astype(np.float64)
    return np.moveaxis((codes * scale).reshape(v.shape), -1, axis)


WIDE = False


def mx_kscale(k):
    if not WIDE:
        return np.ones(k)
    levels = np.array([10, -10, 5, -5, 0])
    a = np.random.permutation(np.resize(levels, k // 512 * 4)).reshape(k // 512, 4)
    idx = np.arange(k)
    return np.exp2(a[idx // 512, idx % 128 // 32])


BF16 = ml_dtypes.bfloat16


def bf(x):
    return np.asarray(x, np.float32).astype(BF16)


def f64(x):
    return np.asarray(x).astype(np.float64)


B, N, D = 24, 512, 256
C = 2 * D
EPS_BN = 1e-5
NEG_SLOPE = 0.01


def bn_lrelu(x, g, b):
    mean = np.mean(x, axis=(0, 2), keepdims=True)
    var = np.var(x, axis=(0, 2), keepdims=True)
    y = (x - mean) / np.sqrt(var + EPS_BN) * g[None, :, None] + b[None, :, None]
    return np.where(y >= 0, y, NEG_SLOPE * y)


def setup_inputs():
    s = mx_kscale(C)
    v = np.random.standard_normal((B, C, N))
    return {"h1": bf(np.where(v >= 0, v, NEG_SLOPE * v) * s[None, :, None]),
            "W2": bf(np.random.standard_normal((D, C)) / np.sqrt(C) / s[None, :]),
            "g2": bf(1.0 + 0.2 * np.random.standard_normal(D)),
            "b2": bf(0.3 * np.random.standard_normal(D))}


def reference(h1, W2, g2, b2):
    z = mxq(f64(W2), 1, "e4m3") @ mxq(f64(h1), 1, "e4m3")
    return np.swapaxes(bn_lrelu(z, f64(g2), f64(b2)), 1, 2)

@@ -1,0 +1,243 @@
+from contextlib import ExitStack
+
+import concourse.mybir as mybir
+from concourse.masks import make_identity
+
+BF16 = mybir.dt.bfloat16
+F32 = mybir.dt.float32
+U32 = mybir.dt.uint32
+U8 = mybir.dt.uint8
+FP8X4 = mybir.dt.float8_e4m3fn_x4
+ACT = mybir.ActivationFunctionType
+ALU = mybir.AluOpType
+AXIS = mybir.AxisListType
+
+P = 128
+PACK = 4
+GRAPHS = 24
+C_IN = 512
+NODES = 512
+C_OUT = 256
+HALVES = C_OUT // P
+NODE_TILES = NODES // P
+RUN = 4
+VECTOR_NODES = 448
+EPS_BN = 1e-5
+NEG_SLOPE = 0.01
+COUNT = GRAPHS * NODES
+
+FLOPS = 2 * GRAPHS * C_OUT * C_IN * NODES
+
+
+def tile_yuyipointupdate_pb_t_kernel(tc, h1, W2, g2, b2, out):
+    nc = tc.nc
+    with ExitStack() as ctx:
+        ctx.enter_context(tc.manual_schedule())
+        keep = ctx.enter_context(tc.tile_pool(name="keep", bufs=1))
+        raw_pool = ctx.enter_context(tc.tile_pool(name="raw", bufs=6))
+        grouped_pool = ctx.enter_context(tc.tile_pool(name="grouped", bufs=3))
+        squares_pool = ctx.enter_context(tc.tile_pool(name="squares", bufs=4))
+        y_pool = ctx.enter_context(tc.tile_pool(name="y", bufs=3))
+        r_pool = ctx.enter_context(tc.tile_pool(name="r", bufs=3))
+        rows_pool = ctx.enter_context(tc.tile_pool(name="rows", bufs=4))
+        z_pool = ctx.enter_context(tc.psum_pool(name="z", bufs=2 * HALVES))
+
+        w_codes = keep.tile([P, C_OUT], U32, align_bytes=64)
+        w_scales = keep.tile([P, C_OUT], U8, align_bytes=64)
+        h_codes = keep.tile([P, GRAPHS, NODES], U32, align_bytes=64)
+        h_scales = keep.tile([P, GRAPHS, NODES], U8, align_bytes=64)
+        sum_sq_parts = keep.tile([P, HALVES, GRAPHS], F32)
+
+        def product(acc, b, h, start, stop):
+            o_cols = slice(h * P, (h + 1) * P)
+            nc.tensor.matmul_mx(
+                out=acc,
+                lhsT=w_codes[:, o_cols].bitcast(FP8X4),
+                lhsT_scale=w_scales[:, o_cols],
+                rhs=h_codes[:, b, :].bitcast(FP8X4),
+                rhs_scale=h_scales[:, b, :],
+                start=start,
+                stop=stop,
+            )
+
+        def regroup(copy, grouped, raw, nodes):
+            copy(
+                out=grouped[:, nodes, :].rearrange("p (c i) j -> p c j i", i=RUN),
+                in_=raw[:, :, nodes].rearrange("p j (c i) -> p c j i", i=RUN),
+            )
+
+        w_rows = keep.tile([P, HALVES, C_IN], BF16)
+        nc.scalar.dma_start(out=w_rows[:], in_=W2.rearrange("(h o) c -> o h c", h=HALVES))
+        gb_rows = keep.tile([P, P], BF16)
+        nc.vector.memset(gb_rows[:], 0.0)
+        nc.scalar.dma_start(out=gb_rows[0:HALVES, :], in_=g2.rearrange("(h o) -> h o", h=HALVES))
+        nc.scalar.dma_start(
+            out=gb_rows[HALVES : 2 * HALVES, :], in_=b2.rearrange("(h o) -> h o", h=HALVES)
+        )
+
+        one = keep.tile([P, 1], F32)
+        nc.vector.memset(one[:], 1.0)
+        warm = keep.tile([P, 1], F32)
+        nc.scalar.activation(out=warm[:], in_=one[:], func=ACT.Sqrt)
+
+        ident_bf16 = keep.tile([P, P], BF16)
+        make_identity(nc, ident_bf16[:])
+        ident_f32 = keep.tile([P, P], F32)
+        make_identity(nc, ident_f32[:])
+
+        with tc.psum_pool(name="early", bufs=1) as early:
+            w_sorted = keep.tile([P, HALVES, PACK, P], BF16)
+            nc.vector.tensor_copy(
+                out=w_sorted[:], in_=w_rows[:].rearrange("o h (p j) -> o h j p", j=PACK)
+            )
+            w_t = early.tile([P, HALVES, PACK, P], BF16)
+            for h in range(HALVES):
+                for j in range(PACK):
+                    nc.tensor.transpose(w_t[:, h, j, :], w_sorted[:, h, j, :], ident_bf16[:])
+            w_grouped = keep.tile([P, HALVES, P, PACK], BF16, align_bytes=64)
+
+            def quantise_w2():
+                nc.vector.tensor_copy(out=w_grouped[:], in_=w_t[:].rearrange("p h j o -> p h o j"))
+                nc.vector.quantize_mx(
+                    out=w_codes[:].bitcast(FP8X4),
+                    scales=w_scales[:],
+                    in_=w_grouped[:].rearrange("p h o j -> p (h o j)"),
+                )
+
+            z_over_graphs = [
+                early.tile([P, NODES], F32, name="z_over_graphs%d" % h) for h in range(HALVES)
+            ]
+            grouped_of = {}
+            z_of = {}
+
+            def load_and_regroup(b):
+                raw = raw_pool.tile([P, PACK, NODES], BF16)
+                nc.sync.dma_start(out=raw[:], in_=h1[b].rearrange("(p j) n -> p j n", j=PACK))
+                grouped = grouped_pool.tile([P, NODES, PACK], BF16, align_bytes=64)
+                regroup(nc.vector.tensor_copy, grouped, raw, slice(0, VECTOR_NODES))
+                regroup(nc.scalar.copy, grouped, raw, slice(VECTOR_NODES, NODES))
+                grouped_of[b] = grouped
+
+            def quantise_and_multiply(b):
+                nc.vector.quantize_mx(
+                    out=h_codes[:, b, :].bitcast(FP8X4),
+                    scales=h_scales[:, b, :],
+                    in_=grouped_of[b][:].rearrange("p n j -> p (n j)"),
+                )
+                for h in range(HALVES):
+                    z = z_pool.tile([P, NODES], F32)
+                    product(z[:], b, h, True, True)
+                    z_of[b, h] = z
+                    product(z_over_graphs[h][:], b, h, b == 0, b == GRAPHS - 1)
+
+            def square_and_sum(b):
+                for h in range(HALVES):
+                    squares = squares_pool.tile([P, NODES], BF16)
+                    nc.scalar.activation(
+                        out=squares[:],
+                        in_=z_of[b, h][:],
+                        func=ACT.Square,
+                        accum_out=sum_sq_parts[:, h, b : b + 1],
+                    )
+
+            for step in range(GRAPHS + 2):
+                if step < GRAPHS:
+                    load_and_regroup(step)
+                if step == 0:
+                    quantise_w2()
+                if 1 <= step <= GRAPHS:
+                    quantise_and_multiply(step - 1)
+                if step >= 2:
+                    square_and_sum(step - 2)
+
+            gb_t = early.tile([P, P], BF16)
+            nc.tensor.transpose(gb_t[:], gb_rows[:], ident_bf16[:])
+            gain_shift = keep.tile([P, 2 * HALVES], F32)
+            nc.vector.tensor_copy(out=gain_shift[:], in_=gb_t[:, 0 : 2 * HALVES])
+
+            sum_z = keep.tile([P, HALVES], F32)
+            for h in range(HALVES):
+                nc.vector.reduce_sum(
+                    out=sum_z[:, h : h + 1], in_=z_over_graphs[h][:], axis=AXIS.X
+                )
+
+        mean = keep.tile([P, HALVES], F32)
+        nc.vector.tensor_scalar_mul(out=mean[:], in0=sum_z[:], scalar1=1.0 / COUNT)
+        mean_sq = keep.tile([P, HALVES], F32)
+        nc.vector.tensor_mul(out=mean_sq[:], in0=mean[:], in1=mean[:])
+        sum_sq = keep.tile([P, HALVES], F32)
+        nc.vector.reduce_sum(out=sum_sq[:], in_=sum_sq_parts[:], axis=AXIS.X)
+        var = keep.tile([P, HALVES], F32)
+        nc.vector.scalar_tensor_tensor(
+            out=var[:], in0=sum_sq[:], scalar=1.0 / COUNT, in1=mean_sq[:],
+            op0=ALU.mult, op1=ALU.subtract,
+        )
+        var_eps = keep.tile([P, HALVES], F32)
+        nc.vector.tensor_scalar(
+            out=var_eps[:], in0=var[:], scalar1=0.0, scalar2=EPS_BN, op0=ALU.max, op1=ALU.add
+        )
+        std = keep.tile([P, HALVES], F32)
+        nc.scalar.activation(out=std[:], in_=var_eps[:], func=ACT.Sqrt)
+        inv_std = keep.tile([P, HALVES], F32)
+        nc.vector.reciprocal(out=inv_std[:], in_=std[:])
+        scale = keep.tile([P, HALVES], F32)
+        nc.vector.tensor_mul(out=scale[:], in0=gain_shift[:, 0:HALVES], in1=inv_std[:])
+        mean_scaled = keep.tile([P, HALVES], F32)
+        nc.vector.tensor_mul(out=mean_scaled[:], in0=mean[:], in1=scale[:])
+        shift = keep.tile([P, HALVES], F32)
+        nc.vector.tensor_sub(
+            out=shift[:], in0=gain_shift[:, HALVES : 2 * HALVES], in1=mean_scaled[:]
+        )
+
+        with tc.psum_pool(name="turned", bufs=4) as turned_pool:
+            y_of = {}
+            r_of = {}
+
+            def multiply_and_normalise(b):
+                y = y_pool.tile([P, HALVES, NODES], F32)
+                for h in range(HALVES):
+                    z = z_pool.tile([P, NODES], F32)
+                    product(z[:], b, h, True, True)
+                    nc.scalar.activation(
+                        out=y[:, h, :],
+                        in_=z[:],
+                        func=ACT.Identity,
+                        scale=scale[:, h : h + 1],
+                        bias=shift[:, h : h + 1],
+                    )
+                y_of[b] = y
+
+            def leaky_relu(b):
+                r = r_pool.tile([P, HALVES, NODES], F32)
+                y_flat = y_of[b][:].rearrange("o h n -> o (h n)")
+                nc.vector.scalar_tensor_tensor(
+                    out=r[:].rearrange("o h n -> o (h n)"),
+                    in0=y_flat, scalar=NEG_SLOPE, in1=y_flat, op0=ALU.mult, op1=ALU.max,
+                )
+                r_of[b] = r
+
+            def turn_and_store(b):
+                rows = rows_pool.tile([P, NODE_TILES, C_OUT], F32)
+                banks = []
+                for pair in range(NODE_TILES // 2):
+                    turned = turned_pool.tile([P, 2, C_OUT], F32)
+                    for k in range(2):
+                        t = 2 * pair + k
+                        for h in range(HALVES):
+                            nc.tensor.transpose(
+                                turned[:, k, h * P : (h + 1) * P],
+                                r_of[b][:, h, t * P : (t + 1) * P],
+                                ident_f32[:],
+                            )
+                    banks.append(turned)
+                nc.scalar.copy(out=rows[:, 0:2, :], in_=banks[0][:])
+                nc.vector.tensor_copy(out=rows[:, 2:4, :], in_=banks[1][:])
+                nc.sync.dma_start(out=out[b].rearrange("(t p) o -> p t o", p=P), in_=rows[:])
+
+            for step in range(GRAPHS + 2):
+                if step < GRAPHS:
+                    multiply_and_normalise(step)
+                if 1 <= step <= GRAPHS:
+                    leaky_relu(step - 1)
+                if step >= 2:
+                    turn_and_store(step - 2)

@@ -21,7 +21,7 @@ C_OUT = 256
 HALVES = C_OUT // P
 NODE_TILES = NODES // P
 RUN = 4
-VECTOR_NODES = 448
+VECTOR_NODES = 416
 EPS_BN = 1e-5
 NEG_SLOPE = 0.01
 COUNT = GRAPHS * NODES
@@ -35,7 +35,7 @@ def tile_yuyipointupdate_pb_t_kernel(tc, h1, W2, g2, b2, out):
         ctx.enter_context(tc.manual_schedule())
         keep = ctx.enter_context(tc.tile_pool(name="keep", bufs=1))
         raw_pool = ctx.enter_context(tc.tile_pool(name="raw", bufs=6))
-        grouped_pool = ctx.enter_context(tc.tile_pool(name="grouped", bufs=3))
+        grouped_pool = ctx.enter_context(tc.tile_pool(name="grouped", bufs=4))
         squares_pool = ctx.enter_context(tc.tile_pool(name="squares", bufs=4))
         y_pool = ctx.enter_context(tc.tile_pool(name="y", bufs=3))
         r_pool = ctx.enter_context(tc.tile_pool(name="r", bufs=3))
@@ -47,6 +47,7 @@ def tile_yuyipointupdate_pb_t_kernel(tc, h1, W2, g2, b2, out):
         h_codes = keep.tile([P, GRAPHS, NODES], U32, align_bytes=64)
         h_scales = keep.tile([P, GRAPHS, NODES], U8, align_bytes=64)
         sum_sq_parts = keep.tile([P, HALVES, GRAPHS], F32)
+        z_of = {}
 
         def product(acc, b, h, start, stop):
             o_cols = slice(h * P, (h + 1) * P)
@@ -87,7 +88,7 @@ def tile_yuyipointupdate_pb_t_kernel(tc, h1, W2, g2, b2, out):
 
         with tc.psum_pool(name="early", bufs=1) as early:
             w_sorted = keep.tile([P, HALVES, PACK, P], BF16)
-            nc.vector.tensor_copy(
+            nc.scalar.copy(
                 out=w_sorted[:], in_=w_rows[:].rearrange("o h (p j) -> o h j p", j=PACK)
             )
             w_t = early.tile([P, HALVES, PACK, P], BF16)
@@ -97,7 +98,7 @@ def tile_yuyipointupdate_pb_t_kernel(tc, h1, W2, g2, b2, out):
             w_grouped = keep.tile([P, HALVES, P, PACK], BF16, align_bytes=64)
 
             def quantise_w2():
-                nc.vector.tensor_copy(out=w_grouped[:], in_=w_t[:].rearrange("p h j o -> p h o j"))
+                nc.scalar.copy(out=w_grouped[:], in_=w_t[:].rearrange("p h j o -> p h o j"))
                 nc.vector.quantize_mx(
                     out=w_codes[:].bitcast(FP8X4),
                     scales=w_scales[:],
@@ -108,7 +109,6 @@ def tile_yuyipointupdate_pb_t_kernel(tc, h1, W2, g2, b2, out):
                 early.tile([P, NODES], F32, name="z_over_graphs%d" % h) for h in range(HALVES)
             ]
             grouped_of = {}
-            z_of = {}
 
             def load_and_regroup(b):
                 raw = raw_pool.tile([P, PACK, NODES], BF16)
@@ -118,12 +118,14 @@ def tile_yuyipointupdate_pb_t_kernel(tc, h1, W2, g2, b2, out):
                 regroup(nc.scalar.copy, grouped, raw, slice(VECTOR_NODES, NODES))
                 grouped_of[b] = grouped
 
-            def quantise_and_multiply(b):
+            def quantise(b):
                 nc.vector.quantize_mx(
                     out=h_codes[:, b, :].bitcast(FP8X4),
                     scales=h_scales[:, b, :],
                     in_=grouped_of[b][:].rearrange("p n j -> p (n j)"),
                 )
+
+            def multiply_for_statistics(b):
                 for h in range(HALVES):
                     z = z_pool.tile([P, NODES], F32)
                     product(z[:], b, h, True, True)
@@ -143,10 +145,12 @@ def tile_yuyipointupdate_pb_t_kernel(tc, h1, W2, g2, b2, out):
             for step in range(GRAPHS + 2):
                 if step < GRAPHS:
                     load_and_regroup(step)
-                if step == 0:
+                if 1 <= step <= GRAPHS:
+                    quantise(step - 1)
+                if step == 1:
                     quantise_w2()
                 if 1 <= step <= GRAPHS:
-                    quantise_and_multiply(step - 1)
+                    multiply_for_statistics(step - 1)
                 if step >= 2:
                     square_and_sum(step - 2)
 
@@ -165,6 +169,11 @@ def tile_yuyipointupdate_pb_t_kernel(tc, h1, W2, g2, b2, out):
         nc.vector.tensor_scalar_mul(out=mean[:], in0=sum_z[:], scalar1=1.0 / COUNT)
         mean_sq = keep.tile([P, HALVES], F32)
         nc.vector.tensor_mul(out=mean_sq[:], in0=mean[:], in1=mean[:])
+        minus_gain_mean = keep.tile([P, HALVES], F32)
+        nc.vector.scalar_tensor_tensor(
+            out=minus_gain_mean[:], in0=mean[:], scalar=-1.0, in1=gain_shift[:, 0:HALVES],
+            op0=ALU.mult, op1=ALU.mult,
+        )
         sum_sq = keep.tile([P, HALVES], F32)
         nc.vector.reduce_sum(out=sum_sq[:], in_=sum_sq_parts[:], axis=AXIS.X)
         var = keep.tile([P, HALVES], F32)
@@ -182,25 +191,34 @@ def tile_yuyipointupdate_pb_t_kernel(tc, h1, W2, g2, b2, out):
         nc.vector.reciprocal(out=inv_std[:], in_=std[:])
         scale = keep.tile([P, HALVES], F32)
         nc.vector.tensor_mul(out=scale[:], in0=gain_shift[:, 0:HALVES], in1=inv_std[:])
-        mean_scaled = keep.tile([P, HALVES], F32)
-        nc.vector.tensor_mul(out=mean_scaled[:], in0=mean[:], in1=scale[:])
         shift = keep.tile([P, HALVES], F32)
-        nc.vector.tensor_sub(
-            out=shift[:], in0=gain_shift[:, HALVES : 2 * HALVES], in1=mean_scaled[:]
-        )
+        for h in range(HALVES):
+            nc.vector.scalar_tensor_tensor(
+                out=shift[:, h : h + 1],
+                in0=minus_gain_mean[:, h : h + 1],
+                scalar=inv_std[:, h : h + 1],
+                in1=gain_shift[:, HALVES + h : HALVES + h + 1],
+                op0=ALU.mult,
+                op1=ALU.add,
+            )
 
         with tc.psum_pool(name="turned", bufs=4) as turned_pool:
             y_of = {}
             r_of = {}
+            banks_of = {}
 
-            def multiply_and_normalise(b):
-                y = y_pool.tile([P, HALVES, NODES], F32)
+            def multiply(b):
                 for h in range(HALVES):
                     z = z_pool.tile([P, NODES], F32)
                     product(z[:], b, h, True, True)
+                    z_of[b, h] = z
+
+            def normalise(b):
+                y = y_pool.tile([P, HALVES, NODES], F32)
+                for h in range(HALVES):
                     nc.scalar.activation(
                         out=y[:, h, :],
-                        in_=z[:],
+                        in_=z_of[b, h][:],
                         func=ACT.Identity,
                         scale=scale[:, h : h + 1],
                         bias=shift[:, h : h + 1],
@@ -216,8 +234,7 @@ def tile_yuyipointupdate_pb_t_kernel(tc, h1, W2, g2, b2, out):
                 )
                 r_of[b] = r
 
-            def turn_and_store(b):
-                rows = rows_pool.tile([P, NODE_TILES, C_OUT], F32)
+            def turn(b):
                 banks = []
                 for pair in range(NODE_TILES // 2):
                     turned = turned_pool.tile([P, 2, C_OUT], F32)
@@ -230,14 +247,23 @@ def tile_yuyipointupdate_pb_t_kernel(tc, h1, W2, g2, b2, out):
                                 ident_f32[:],
                             )
                     banks.append(turned)
-                nc.scalar.copy(out=rows[:, 0:2, :], in_=banks[0][:])
-                nc.vector.tensor_copy(out=rows[:, 2:4, :], in_=banks[1][:])
+                banks_of[b] = banks
+
+            def empty_and_store(b):
+                rows = rows_pool.tile([P, NODE_TILES, C_OUT], F32)
+                nc.scalar.copy(out=rows[:, 0:2, :], in_=banks_of[b][0][:])
+                nc.vector.tensor_copy(out=rows[:, 2:4, :], in_=banks_of[b][1][:])
                 nc.sync.dma_start(out=out[b].rearrange("(t p) o -> p t o", p=P), in_=rows[:])
 
+            multiply(0)
             for step in range(GRAPHS + 2):
+                if step >= 2:
+                    turn(step - 2)
+                if step + 1 < GRAPHS:
+                    multiply(step + 1)
                 if step < GRAPHS:
-                    multiply_and_normalise(step)
+                    normalise(step)
                 if 1 <= step <= GRAPHS:
                     leaky_relu(step - 1)
                 if step >= 2:
-                    turn_and_store(step - 2)
+                    empty_and_store(step - 2)

@@ -21,7 +21,8 @@ C_OUT = 256
 HALVES = C_OUT // P
 NODE_TILES = NODES // P
 RUN = 4
-VECTOR_NODES = 416
+SCALAR_EVERY = 6
+SCALAR_LEAD = 2
 EPS_BN = 1e-5
 NEG_SLOPE = 0.01
 COUNT = GRAPHS * NODES
@@ -34,12 +35,11 @@ def tile_yuyipointupdate_pb_t_kernel(tc, h1, W2, g2, b2, out):
     with ExitStack() as ctx:
         ctx.enter_context(tc.manual_schedule())
         keep = ctx.enter_context(tc.tile_pool(name="keep", bufs=1))
-        raw_pool = ctx.enter_context(tc.tile_pool(name="raw", bufs=6))
         grouped_pool = ctx.enter_context(tc.tile_pool(name="grouped", bufs=4))
         squares_pool = ctx.enter_context(tc.tile_pool(name="squares", bufs=4))
         y_pool = ctx.enter_context(tc.tile_pool(name="y", bufs=3))
         r_pool = ctx.enter_context(tc.tile_pool(name="r", bufs=3))
-        rows_pool = ctx.enter_context(tc.tile_pool(name="rows", bufs=4))
+        rows_pool = ctx.enter_context(tc.tile_pool(name="rows", bufs=8))
         z_pool = ctx.enter_context(tc.psum_pool(name="z", bufs=2 * HALVES))
 
         w_codes = keep.tile([P, C_OUT], U32, align_bytes=64)
@@ -48,6 +48,10 @@ def tile_yuyipointupdate_pb_t_kernel(tc, h1, W2, g2, b2, out):
         h_scales = keep.tile([P, GRAPHS, NODES], U8, align_bytes=64)
         sum_sq_parts = keep.tile([P, HALVES, GRAPHS], F32)
         z_of = {}
+
+        raw = keep.tile([P, GRAPHS, PACK, NODES], BF16)
+        for b in range(GRAPHS):
+            nc.sync.dma_start(out=raw[:, b, :, :], in_=h1[b].rearrange("(p j) n -> p j n", j=PACK))
 
         def product(acc, b, h, start, stop):
             o_cols = slice(h * P, (h + 1) * P)
@@ -59,12 +63,6 @@ def tile_yuyipointupdate_pb_t_kernel(tc, h1, W2, g2, b2, out):
                 rhs_scale=h_scales[:, b, :],
                 start=start,
                 stop=stop,
-            )
-
-        def regroup(copy, grouped, raw, nodes):
-            copy(
-                out=grouped[:, nodes, :].rearrange("p (c i) j -> p c j i", i=RUN),
-                in_=raw[:, :, nodes].rearrange("p j (c i) -> p c j i", i=RUN),
             )
 
         w_rows = keep.tile([P, HALVES, C_IN], BF16)
@@ -96,26 +94,34 @@ def tile_yuyipointupdate_pb_t_kernel(tc, h1, W2, g2, b2, out):
                 for j in range(PACK):
                     nc.tensor.transpose(w_t[:, h, j, :], w_sorted[:, h, j, :], ident_bf16[:])
             w_grouped = keep.tile([P, HALVES, P, PACK], BF16, align_bytes=64)
+            nc.scalar.copy(out=w_grouped[:], in_=w_t[:].rearrange("p h j o -> p h o j"))
 
-            def quantise_w2():
-                nc.scalar.copy(out=w_grouped[:], in_=w_t[:].rearrange("p h j o -> p h o j"))
+            gb_t = early.tile([P, P], BF16)
+            nc.tensor.transpose(gb_t[:], gb_rows[:], ident_bf16[:])
+            gain_shift = keep.tile([P, 2 * HALVES], F32)
+
+            def finish_small_operands():
                 nc.vector.quantize_mx(
                     out=w_codes[:].bitcast(FP8X4),
                     scales=w_scales[:],
                     in_=w_grouped[:].rearrange("p h o j -> p (h o j)"),
                 )
+                nc.vector.tensor_copy(out=gain_shift[:], in_=gb_t[:, 0 : 2 * HALVES])
 
             z_over_graphs = [
                 early.tile([P, NODES], F32, name="z_over_graphs%d" % h) for h in range(HALVES)
             ]
             grouped_of = {}
 
-            def load_and_regroup(b):
-                raw = raw_pool.tile([P, PACK, NODES], BF16)
-                nc.sync.dma_start(out=raw[:], in_=h1[b].rearrange("(p j) n -> p j n", j=PACK))
+            def scalar_regroups(b):
+                return b % SCALAR_EVERY == SCALAR_LEAD
+
+            def regroup(copy, b):
                 grouped = grouped_pool.tile([P, NODES, PACK], BF16, align_bytes=64)
-                regroup(nc.vector.tensor_copy, grouped, raw, slice(0, VECTOR_NODES))
-                regroup(nc.scalar.copy, grouped, raw, slice(VECTOR_NODES, NODES))
+                copy(
+                    out=grouped[:].rearrange("p (c i) j -> p c j i", i=RUN),
+                    in_=raw[:, b, :, :].rearrange("p j (c i) -> p c j i", i=RUN),
+                )
                 grouped_of[b] = grouped
 
             def quantise(b):
@@ -127,10 +133,10 @@ def tile_yuyipointupdate_pb_t_kernel(tc, h1, W2, g2, b2, out):
 
             def multiply_for_statistics(b):
                 for h in range(HALVES):
+                    product(z_over_graphs[h][:], b, h, b == 0, b == GRAPHS - 1)
                     z = z_pool.tile([P, NODES], F32)
                     product(z[:], b, h, True, True)
                     z_of[b, h] = z
-                    product(z_over_graphs[h][:], b, h, b == 0, b == GRAPHS - 1)
 
             def square_and_sum(b):
                 for h in range(HALVES):
@@ -143,21 +149,18 @@ def tile_yuyipointupdate_pb_t_kernel(tc, h1, W2, g2, b2, out):
                     )
 
             for step in range(GRAPHS + 2):
-                if step < GRAPHS:
-                    load_and_regroup(step)
+                if step + SCALAR_LEAD < GRAPHS and scalar_regroups(step + SCALAR_LEAD):
+                    regroup(nc.scalar.copy, step + SCALAR_LEAD)
+                if step < GRAPHS and not scalar_regroups(step):
+                    regroup(nc.vector.tensor_copy, step)
                 if 1 <= step <= GRAPHS:
                     quantise(step - 1)
                 if step == 1:
-                    quantise_w2()
+                    finish_small_operands()
                 if 1 <= step <= GRAPHS:
                     multiply_for_statistics(step - 1)
                 if step >= 2:
                     square_and_sum(step - 2)
-
-            gb_t = early.tile([P, P], BF16)
-            nc.tensor.transpose(gb_t[:], gb_rows[:], ident_bf16[:])
-            gain_shift = keep.tile([P, 2 * HALVES], F32)
-            nc.vector.tensor_copy(out=gain_shift[:], in_=gb_t[:, 0 : 2 * HALVES])
 
             sum_z = keep.tile([P, HALVES], F32)
             for h in range(HALVES):
@@ -169,11 +172,6 @@ def tile_yuyipointupdate_pb_t_kernel(tc, h1, W2, g2, b2, out):
         nc.vector.tensor_scalar_mul(out=mean[:], in0=sum_z[:], scalar1=1.0 / COUNT)
         mean_sq = keep.tile([P, HALVES], F32)
         nc.vector.tensor_mul(out=mean_sq[:], in0=mean[:], in1=mean[:])
-        minus_gain_mean = keep.tile([P, HALVES], F32)
-        nc.vector.scalar_tensor_tensor(
-            out=minus_gain_mean[:], in0=mean[:], scalar=-1.0, in1=gain_shift[:, 0:HALVES],
-            op0=ALU.mult, op1=ALU.mult,
-        )
         sum_sq = keep.tile([P, HALVES], F32)
         nc.vector.reduce_sum(out=sum_sq[:], in_=sum_sq_parts[:], axis=AXIS.X)
         var = keep.tile([P, HALVES], F32)
@@ -187,6 +185,11 @@ def tile_yuyipointupdate_pb_t_kernel(tc, h1, W2, g2, b2, out):
         )
         std = keep.tile([P, HALVES], F32)
         nc.scalar.activation(out=std[:], in_=var_eps[:], func=ACT.Sqrt)
+        minus_gain_mean = keep.tile([P, HALVES], F32)
+        nc.vector.scalar_tensor_tensor(
+            out=minus_gain_mean[:], in0=mean[:], scalar=-1.0, in1=gain_shift[:, 0:HALVES],
+            op0=ALU.mult, op1=ALU.mult,
+        )
         inv_std = keep.tile([P, HALVES], F32)
         nc.vector.reciprocal(out=inv_std[:], in_=std[:])
         scale = keep.tile([P, HALVES], F32)
@@ -250,10 +253,11 @@ def tile_yuyipointupdate_pb_t_kernel(tc, h1, W2, g2, b2, out):
                 banks_of[b] = banks
 
             def empty_and_store(b):
-                rows = rows_pool.tile([P, NODE_TILES, C_OUT], F32)
-                nc.scalar.copy(out=rows[:, 0:2, :], in_=banks_of[b][0][:])
-                nc.vector.tensor_copy(out=rows[:, 2:4, :], in_=banks_of[b][1][:])
-                nc.sync.dma_start(out=out[b].rearrange("(t p) o -> p t o", p=P), in_=rows[:])
+                out_tiles = out[b].rearrange("(t p) o -> p t o", p=P)
+                for pair, copy in enumerate((nc.scalar.copy, nc.vector.tensor_copy)):
+                    rows = rows_pool.tile([P, 2, C_OUT], F32)
+                    copy(out=rows[:], in_=banks_of[b][pair][:])
+                    nc.sync.dma_start(out=out_tiles[:, 2 * pair : 2 * pair + 2, :], in_=rows[:])
 
             multiply(0)
             for step in range(GRAPHS + 2):

@@ -22,9 +22,18 @@ HALVES = C_OUT // P
 NODE_TILES = NODES // P
 RUN = 4
 SCALAR_EVERY = 6
+GAIN_STEP = 8
 SCALAR_LEAD = 2
+HALF_NODES = NODES // 2
+LEFT, RIGHT, WHOLE = slice(0, HALF_NODES), slice(HALF_NODES, NODES), slice(0, NODES)
+PIECES = (
+    [(0, LEFT), (0, RIGHT)]
+    + [(b, WHOLE) for b in range(1, GRAPHS - 1)]
+    + [(GRAPHS - 1, LEFT), (GRAPHS - 1, RIGHT)]
+)
 EPS_BN = 1e-5
 NEG_SLOPE = 0.01
+SUM_NODES = 128
 COUNT = GRAPHS * NODES
 
 FLOPS = 2 * GRAPHS * C_OUT * C_IN * NODES
@@ -46,21 +55,22 @@ def tile_yuyipointupdate_pb_t_kernel(tc, h1, W2, g2, b2, out):
         w_scales = keep.tile([P, C_OUT], U8, align_bytes=64)
         h_codes = keep.tile([P, GRAPHS, NODES], U32, align_bytes=64)
         h_scales = keep.tile([P, GRAPHS, NODES], U8, align_bytes=64)
-        sum_sq_parts = keep.tile([P, HALVES, GRAPHS], F32)
+        sum_sq_parts = keep.tile([P, HALVES, len(PIECES)], F32)
         z_of = {}
 
         raw = keep.tile([P, GRAPHS, PACK, NODES], BF16)
-        for b in range(GRAPHS):
-            nc.sync.dma_start(out=raw[:, b, :, :], in_=h1[b].rearrange("(p j) n -> p j n", j=PACK))
+        for b, nodes in PIECES:
+            h1_b = h1[b].rearrange("(p j) n -> p j n", j=PACK)
+            nc.sync.dma_start(out=raw[:, b, :, nodes], in_=h1_b[:, :, nodes])
 
-        def product(acc, b, h, start, stop):
+        def product(acc, b, h, n_cols, start, stop):
             o_cols = slice(h * P, (h + 1) * P)
             nc.tensor.matmul_mx(
                 out=acc,
                 lhsT=w_codes[:, o_cols].bitcast(FP8X4),
                 lhsT_scale=w_scales[:, o_cols],
-                rhs=h_codes[:, b, :].bitcast(FP8X4),
-                rhs_scale=h_scales[:, b, :],
+                rhs=h_codes[:, b, n_cols].bitcast(FP8X4),
+                rhs_scale=h_scales[:, b, n_cols],
                 start=start,
                 stop=stop,
             )
@@ -77,7 +87,7 @@ def tile_yuyipointupdate_pb_t_kernel(tc, h1, W2, g2, b2, out):
         one = keep.tile([P, 1], F32)
         nc.vector.memset(one[:], 1.0)
         warm = keep.tile([P, 1], F32)
-        nc.scalar.activation(out=warm[:], in_=one[:], func=ACT.Sqrt)
+        nc.scalar.activation(out=warm[:], in_=one[:], func=ACT.Abs_reciprocal_sqrt)
 
         ident_bf16 = keep.tile([P, P], BF16)
         make_identity(nc, ident_bf16[:])
@@ -85,124 +95,136 @@ def tile_yuyipointupdate_pb_t_kernel(tc, h1, W2, g2, b2, out):
         make_identity(nc, ident_f32[:])
 
         with tc.psum_pool(name="early", bufs=1) as early:
-            w_sorted = keep.tile([P, HALVES, PACK, P], BF16)
-            nc.scalar.copy(
-                out=w_sorted[:], in_=w_rows[:].rearrange("o h (p j) -> o h j p", j=PACK)
-            )
             w_t = early.tile([P, HALVES, PACK, P], BF16)
             for h in range(HALVES):
                 for j in range(PACK):
-                    nc.tensor.transpose(w_t[:, h, j, :], w_sorted[:, h, j, :], ident_bf16[:])
+                    nc.tensor.transpose(w_t[:, h, j, :], w_rows[:, h, j::PACK], ident_bf16[:])
             w_grouped = keep.tile([P, HALVES, P, PACK], BF16, align_bytes=64)
             nc.scalar.copy(out=w_grouped[:], in_=w_t[:].rearrange("p h j o -> p h o j"))
 
             gb_t = early.tile([P, P], BF16)
-            nc.tensor.transpose(gb_t[:], gb_rows[:], ident_bf16[:])
             gain_shift = keep.tile([P, 2 * HALVES], F32)
 
-            def finish_small_operands():
+            def quantise_weights():
                 nc.vector.quantize_mx(
                     out=w_codes[:].bitcast(FP8X4),
                     scales=w_scales[:],
                     in_=w_grouped[:].rearrange("p h o j -> p (h o j)"),
                 )
-                nc.vector.tensor_copy(out=gain_shift[:], in_=gb_t[:, 0 : 2 * HALVES])
 
-            z_over_graphs = [
-                early.tile([P, NODES], F32, name="z_over_graphs%d" % h) for h in range(HALVES)
+            node_sums = [
+                early.tile([P, SUM_NODES], F32, name="node_sums%d" % h) for h in range(HALVES)
             ]
+
             grouped_of = {}
 
-            def scalar_regroups(b):
-                return b % SCALAR_EVERY == SCALAR_LEAD
+            def scalar_regroups(i):
+                return i < len(PIECES) and PIECES[i][0] % SCALAR_EVERY == SCALAR_LEAD
 
-            def regroup(copy, b):
+            def regroup(copy, i):
+                b, nodes = PIECES[i]
                 grouped = grouped_pool.tile([P, NODES, PACK], BF16, align_bytes=64)
                 copy(
-                    out=grouped[:].rearrange("p (c i) j -> p c j i", i=RUN),
-                    in_=raw[:, b, :, :].rearrange("p j (c i) -> p c j i", i=RUN),
+                    out=grouped[:, nodes, :].rearrange("p (c i) j -> p c j i", i=RUN),
+                    in_=raw[:, b, :, nodes].rearrange("p j (c i) -> p c j i", i=RUN),
                 )
-                grouped_of[b] = grouped
+                grouped_of[i] = grouped
 
-            def quantise(b):
+            def quantise(i):
+                b, nodes = PIECES[i]
                 nc.vector.quantize_mx(
-                    out=h_codes[:, b, :].bitcast(FP8X4),
-                    scales=h_scales[:, b, :],
-                    in_=grouped_of[b][:].rearrange("p n j -> p (n j)"),
+                    out=h_codes[:, b, nodes].bitcast(FP8X4),
+                    scales=h_scales[:, b, nodes],
+                    in_=grouped_of[i][:, nodes, :].rearrange("p n j -> p (n j)"),
                 )
 
-            def multiply_for_statistics(b):
+            def multiply_for_statistics(i):
+                b, nodes = PIECES[i]
                 for h in range(HALVES):
-                    product(z_over_graphs[h][:], b, h, b == 0, b == GRAPHS - 1)
                     z = z_pool.tile([P, NODES], F32)
-                    product(z[:], b, h, True, True)
-                    z_of[b, h] = z
+                    product(z[:, nodes], b, h, nodes, True, True)
+                    z_of[i, h] = z
+                for h in range(HALVES):
+                    for n in range(nodes.start, nodes.stop, SUM_NODES):
+                        product(
+                            node_sums[h][:], b, h, slice(n, n + SUM_NODES),
+                            b == 0 and n == 0, b == GRAPHS - 1 and n + SUM_NODES == NODES,
+                        )
 
-            def square_and_sum(b):
+            def square_and_sum(i):
+                nodes = PIECES[i][1]
                 for h in range(HALVES):
                     squares = squares_pool.tile([P, NODES], BF16)
                     nc.scalar.activation(
-                        out=squares[:],
-                        in_=z_of[b, h][:],
+                        out=squares[:, nodes],
+                        in_=z_of[i, h][:, nodes],
                         func=ACT.Square,
-                        accum_out=sum_sq_parts[:, h, b : b + 1],
+                        accum_out=sum_sq_parts[:, h, i : i + 1],
                     )
 
-            for step in range(GRAPHS + 2):
-                if step + SCALAR_LEAD < GRAPHS and scalar_regroups(step + SCALAR_LEAD):
+            for step in range(len(PIECES) + 2):
+                if scalar_regroups(step + SCALAR_LEAD):
                     regroup(nc.scalar.copy, step + SCALAR_LEAD)
-                if step < GRAPHS and not scalar_regroups(step):
-                    regroup(nc.vector.tensor_copy, step)
-                if 1 <= step <= GRAPHS:
+                if 1 <= step <= 2:
                     quantise(step - 1)
-                if step == 1:
-                    finish_small_operands()
-                if 1 <= step <= GRAPHS:
+                if step < len(PIECES) and not scalar_regroups(step):
+                    regroup(nc.vector.tensor_copy, step)
+                if 3 <= step <= len(PIECES):
+                    quantise(step - 1)
+                if step == 2:
+                    quantise_weights()
+                    multiply_for_statistics(0)
+                if 2 <= step <= len(PIECES):
                     multiply_for_statistics(step - 1)
+                if step == GAIN_STEP:
+                    nc.tensor.transpose(gb_t[:], gb_rows[:], ident_bf16[:])
+                if step == GAIN_STEP + 1:
+                    nc.vector.tensor_copy(out=gain_shift[:], in_=gb_t[:, 0 : 2 * HALVES])
                 if step >= 2:
                     square_and_sum(step - 2)
 
             sum_z = keep.tile([P, HALVES], F32)
             for h in range(HALVES):
-                nc.vector.reduce_sum(
-                    out=sum_z[:, h : h + 1], in_=z_over_graphs[h][:], axis=AXIS.X
-                )
+                nc.vector.reduce_sum(out=sum_z[:, h : h + 1], in_=node_sums[h][:], axis=AXIS.X)
 
         mean = keep.tile([P, HALVES], F32)
         nc.vector.tensor_scalar_mul(out=mean[:], in0=sum_z[:], scalar1=1.0 / COUNT)
         mean_sq = keep.tile([P, HALVES], F32)
         nc.vector.tensor_mul(out=mean_sq[:], in0=mean[:], in1=mean[:])
-        sum_sq = keep.tile([P, HALVES], F32)
-        nc.vector.reduce_sum(out=sum_sq[:], in_=sum_sq_parts[:], axis=AXIS.X)
-        var = keep.tile([P, HALVES], F32)
-        nc.vector.scalar_tensor_tensor(
-            out=var[:], in0=sum_sq[:], scalar=1.0 / COUNT, in1=mean_sq[:],
-            op0=ALU.mult, op1=ALU.subtract,
-        )
-        var_eps = keep.tile([P, HALVES], F32)
+        eps_minus_mean_sq = keep.tile([P, HALVES], F32)
         nc.vector.tensor_scalar(
-            out=var_eps[:], in0=var[:], scalar1=0.0, scalar2=EPS_BN, op0=ALU.max, op1=ALU.add
+            out=eps_minus_mean_sq[:], in0=mean_sq[:], scalar1=-1.0, scalar2=EPS_BN,
+            op0=ALU.mult, op1=ALU.add,
         )
-        std = keep.tile([P, HALVES], F32)
-        nc.scalar.activation(out=std[:], in_=var_eps[:], func=ACT.Sqrt)
         minus_gain_mean = keep.tile([P, HALVES], F32)
         nc.vector.scalar_tensor_tensor(
             out=minus_gain_mean[:], in0=mean[:], scalar=-1.0, in1=gain_shift[:, 0:HALVES],
             op0=ALU.mult, op1=ALU.mult,
         )
+        parts_copy = keep.tile([P, HALVES, len(PIECES)], F32)
+        sum_sq = keep.tile([P, HALVES], F32)
         inv_std = keep.tile([P, HALVES], F32)
-        nc.vector.reciprocal(out=inv_std[:], in_=std[:])
         scale = keep.tile([P, HALVES], F32)
-        nc.vector.tensor_mul(out=scale[:], in0=gain_shift[:, 0:HALVES], in1=inv_std[:])
         shift = keep.tile([P, HALVES], F32)
         for h in range(HALVES):
-            nc.vector.scalar_tensor_tensor(
-                out=shift[:, h : h + 1],
-                in0=minus_gain_mean[:, h : h + 1],
-                scalar=inv_std[:, h : h + 1],
-                in1=gain_shift[:, HALVES + h : HALVES + h + 1],
-                op0=ALU.mult,
-                op1=ALU.add,
+            nc.scalar.activation(
+                out=parts_copy[:, h, :], in_=sum_sq_parts[:, h, :], func=ACT.Identity,
+                accum_out=sum_sq[:, h : h + 1],
+            )
+        for h in range(HALVES):
+            nc.scalar.activation(
+                out=inv_std[:, h : h + 1], in_=sum_sq[:, h : h + 1], func=ACT.Abs_reciprocal_sqrt,
+                scale=1.0 / COUNT, bias=eps_minus_mean_sq[:, h : h + 1],
+            )
+        for h in range(HALVES):
+            nc.scalar.activation(
+                out=scale[:, h : h + 1], in_=gain_shift[:, h : h + 1], func=ACT.Copy,
+                scale=inv_std[:, h : h + 1],
+            )
+            nc.scalar.activation(
+                out=shift[:, h : h + 1], in_=minus_gain_mean[:, h : h + 1], func=ACT.Identity,
+                scale=inv_std[:, h : h + 1],
+                bias=gain_shift[:, HALVES + h : HALVES + h + 1],
             )
 
         with tc.psum_pool(name="turned", bufs=4) as turned_pool:
@@ -213,7 +235,7 @@ def tile_yuyipointupdate_pb_t_kernel(tc, h1, W2, g2, b2, out):
             def multiply(b):
                 for h in range(HALVES):
                     z = z_pool.tile([P, NODES], F32)
-                    product(z[:], b, h, True, True)
+                    product(z[:], b, h, slice(0, NODES), True, True)
                     z_of[b, h] = z
 
             def normalise(b):

@@ -21,7 +21,7 @@ C_OUT = 256
 HALVES = C_OUT // P
 NODE_TILES = NODES // P
 RUN = 4
-SCALAR_EVERY = 6
+SCALAR_EVERY = 8
 GAIN_STEP = 8
 SCALAR_LEAD = 2
 HALF_NODES = NODES // 2
@@ -55,7 +55,7 @@ def tile_yuyipointupdate_pb_t_kernel(tc, h1, W2, g2, b2, out):
         w_scales = keep.tile([P, C_OUT], U8, align_bytes=64)
         h_codes = keep.tile([P, GRAPHS, NODES], U32, align_bytes=64)
         h_scales = keep.tile([P, GRAPHS, NODES], U8, align_bytes=64)
-        sum_sq_parts = keep.tile([P, HALVES, len(PIECES)], F32)
+        sum_sq_parts = keep.tile([P, HALVES, len(PIECES) + 2], F32)
         z_of = {}
 
         raw = keep.tile([P, GRAPHS, PACK, NODES], BF16)
@@ -86,6 +86,10 @@ def tile_yuyipointupdate_pb_t_kernel(tc, h1, W2, g2, b2, out):
 
         one = keep.tile([P, 1], F32)
         nc.vector.memset(one[:], 1.0)
+        nc.vector.tensor_scalar_mul(
+            out=sum_sq_parts[:, :, len(PIECES) + 1], in0=one[:].to_broadcast([P, HALVES]),
+            scalar1=EPS_BN * COUNT,
+        )
         warm = keep.tile([P, 1], F32)
         nc.scalar.activation(out=warm[:], in_=one[:], func=ACT.Abs_reciprocal_sqrt)
 
@@ -178,7 +182,7 @@ def tile_yuyipointupdate_pb_t_kernel(tc, h1, W2, g2, b2, out):
                     multiply_for_statistics(step - 1)
                 if step == GAIN_STEP:
                     nc.tensor.transpose(gb_t[:], gb_rows[:], ident_bf16[:])
-                if step == GAIN_STEP + 1:
+                if step == GAIN_STEP + 3:
                     nc.vector.tensor_copy(out=gain_shift[:], in_=gb_t[:, 0 : 2 * HALVES])
                 if step >= 2:
                     square_and_sum(step - 2)
@@ -187,36 +191,30 @@ def tile_yuyipointupdate_pb_t_kernel(tc, h1, W2, g2, b2, out):
             for h in range(HALVES):
                 nc.vector.reduce_sum(out=sum_z[:, h : h + 1], in_=node_sums[h][:], axis=AXIS.X)
 
-        mean = keep.tile([P, HALVES], F32)
-        nc.vector.tensor_scalar_mul(out=mean[:], in0=sum_z[:], scalar1=1.0 / COUNT)
-        mean_sq = keep.tile([P, HALVES], F32)
-        nc.vector.tensor_mul(out=mean_sq[:], in0=mean[:], in1=mean[:])
-        eps_minus_mean_sq = keep.tile([P, HALVES], F32)
-        nc.vector.tensor_scalar(
-            out=eps_minus_mean_sq[:], in0=mean_sq[:], scalar1=-1.0, scalar2=EPS_BN,
-            op0=ALU.mult, op1=ALU.add,
+        nc.vector.scalar_tensor_tensor(
+            out=sum_sq_parts[:, :, len(PIECES)], in0=sum_z[:], scalar=-1.0 / COUNT, in1=sum_z[:],
+            op0=ALU.mult, op1=ALU.mult,
         )
         minus_gain_mean = keep.tile([P, HALVES], F32)
         nc.vector.scalar_tensor_tensor(
-            out=minus_gain_mean[:], in0=mean[:], scalar=-1.0, in1=gain_shift[:, 0:HALVES],
+            out=minus_gain_mean[:], in0=sum_z[:], scalar=-1.0 / COUNT, in1=gain_shift[:, 0:HALVES],
             op0=ALU.mult, op1=ALU.mult,
         )
-        parts_copy = keep.tile([P, HALVES, len(PIECES)], F32)
-        sum_sq = keep.tile([P, HALVES], F32)
+        parts_copy = keep.tile([P, HALVES, len(PIECES) + 2], F32)
+        var_eps_sum = keep.tile([P, HALVES], F32)
         inv_std = keep.tile([P, HALVES], F32)
         scale = keep.tile([P, HALVES], F32)
         shift = keep.tile([P, HALVES], F32)
         for h in range(HALVES):
             nc.scalar.activation(
                 out=parts_copy[:, h, :], in_=sum_sq_parts[:, h, :], func=ACT.Identity,
-                accum_out=sum_sq[:, h : h + 1],
+                accum_out=var_eps_sum[:, h : h + 1],
             )
-        for h in range(HALVES):
-            nc.scalar.activation(
-                out=inv_std[:, h : h + 1], in_=sum_sq[:, h : h + 1], func=ACT.Abs_reciprocal_sqrt,
-                scale=1.0 / COUNT, bias=eps_minus_mean_sq[:, h : h + 1],
-            )
-        for h in range(HALVES):
+        nc.scalar.activation(
+            out=inv_std[:], in_=var_eps_sum[:], func=ACT.Abs_reciprocal_sqrt, scale=1.0 / COUNT
+        )
+
+        for h in reversed(range(HALVES)):
             nc.scalar.activation(
                 out=scale[:, h : h + 1], in_=gain_shift[:, h : h + 1], func=ACT.Copy,
                 scale=inv_std[:, h : h + 1],
@@ -241,6 +239,12 @@ def tile_yuyipointupdate_pb_t_kernel(tc, h1, W2, g2, b2, out):
             def normalise(b):
                 y = y_pool.tile([P, HALVES, NODES], F32)
                 for h in range(HALVES):
+                    if (b, h) == (0, 1):
+                        nc.vector.tensor_scalar(
+                            out=y[:, h, :], in0=z_early[:], scalar1=scale[:, h : h + 1],
+                            scalar2=shift[:, h : h + 1], op0=ALU.mult, op1=ALU.add,
+                        )
+                        continue
                     nc.scalar.activation(
                         out=y[:, h, :],
                         in_=z_of[b, h][:],
@@ -252,12 +256,19 @@ def tile_yuyipointupdate_pb_t_kernel(tc, h1, W2, g2, b2, out):
 
             def leaky_relu(b):
                 r = r_pool.tile([P, HALVES, NODES], F32)
-                y_flat = y_of[b][:].rearrange("o h n -> o (h n)")
-                nc.vector.scalar_tensor_tensor(
-                    out=r[:].rearrange("o h n -> o (h n)"),
-                    in0=y_flat, scalar=NEG_SLOPE, in1=y_flat, op0=ALU.mult, op1=ALU.max,
-                )
                 r_of[b] = r
+                if b == 0:
+                    parts = [(slice(1, 2), WHOLE), (slice(0, 1), WHOLE)]
+                elif b == GRAPHS - 1:
+                    parts = [(slice(0, HALVES), LEFT), (slice(0, HALVES), RIGHT)]
+                else:
+                    parts = [(slice(0, HALVES), WHOLE)]
+                for halves, nodes in parts:
+                    y = y_of[b][:, halves, nodes]
+                    nc.vector.scalar_tensor_tensor(
+                        out=r[:, halves, nodes], in0=y, scalar=NEG_SLOPE, in1=y,
+                        op0=ALU.mult, op1=ALU.max,
+                    )
 
             def turn(b):
                 banks = []
@@ -276,12 +287,15 @@ def tile_yuyipointupdate_pb_t_kernel(tc, h1, W2, g2, b2, out):
 
             def empty_and_store(b):
                 out_tiles = out[b].rearrange("(t p) o -> p t o", p=P)
-                for pair, copy in enumerate((nc.scalar.copy, nc.vector.tensor_copy)):
+                second = nc.scalar.copy if b == GRAPHS - 3 else nc.vector.tensor_copy
+                for pair, copy in enumerate((nc.scalar.copy, second)):
                     rows = rows_pool.tile([P, 2, C_OUT], F32)
                     copy(out=rows[:], in_=banks_of[b][pair][:])
                     nc.sync.dma_start(out=out_tiles[:, 2 * pair : 2 * pair + 2, :], in_=rows[:])
 
             multiply(0)
+            z_early = y_pool.tile([P, NODES], F32)
+            nc.vector.tensor_copy(out=z_early[:], in_=z_of[0, 1][:])
             for step in range(GRAPHS + 2):
                 if step >= 2:
                     turn(step - 2)

@@ -21,7 +21,7 @@ C_OUT = 256
 HALVES = C_OUT // P
 NODE_TILES = NODES // P
 RUN = 4
-SCALAR_EVERY = 8
+SCALAR_EVERY = 6
 GAIN_STEP = 8
 SCALAR_LEAD = 2
 HALF_NODES = NODES // 2
@@ -31,6 +31,8 @@ PIECES = (
     + [(b, WHOLE) for b in range(1, GRAPHS - 1)]
     + [(GRAPHS - 1, LEFT), (GRAPHS - 1, RIGHT)]
 )
+LAST_WHOLE = len(PIECES) - 3
+KEEP_CLOCK = 4
 EPS_BN = 1e-5
 NEG_SLOPE = 0.01
 SUM_NODES = 128
@@ -44,12 +46,8 @@ def tile_yuyipointupdate_pb_t_kernel(tc, h1, W2, g2, b2, out):
     with ExitStack() as ctx:
         ctx.enter_context(tc.manual_schedule())
         keep = ctx.enter_context(tc.tile_pool(name="keep", bufs=1))
-        grouped_pool = ctx.enter_context(tc.tile_pool(name="grouped", bufs=4))
-        squares_pool = ctx.enter_context(tc.tile_pool(name="squares", bufs=4))
-        y_pool = ctx.enter_context(tc.tile_pool(name="y", bufs=3))
-        r_pool = ctx.enter_context(tc.tile_pool(name="r", bufs=3))
-        rows_pool = ctx.enter_context(tc.tile_pool(name="rows", bufs=8))
         z_pool = ctx.enter_context(tc.psum_pool(name="z", bufs=2 * HALVES))
+        spare_pool = ctx.enter_context(tc.psum_pool(name="spare", bufs=HALVES))
 
         w_codes = keep.tile([P, C_OUT], U32, align_bytes=64)
         w_scales = keep.tile([P, C_OUT], U8, align_bytes=64)
@@ -57,11 +55,6 @@ def tile_yuyipointupdate_pb_t_kernel(tc, h1, W2, g2, b2, out):
         h_scales = keep.tile([P, GRAPHS, NODES], U8, align_bytes=64)
         sum_sq_parts = keep.tile([P, HALVES, len(PIECES) + 2], F32)
         z_of = {}
-
-        raw = keep.tile([P, GRAPHS, PACK, NODES], BF16)
-        for b, nodes in PIECES:
-            h1_b = h1[b].rearrange("(p j) n -> p j n", j=PACK)
-            nc.sync.dma_start(out=raw[:, b, :, nodes], in_=h1_b[:, :, nodes])
 
         def product(acc, b, h, n_cols, start, stop):
             o_cols = slice(h * P, (h + 1) * P)
@@ -98,15 +91,28 @@ def tile_yuyipointupdate_pb_t_kernel(tc, h1, W2, g2, b2, out):
         ident_f32 = keep.tile([P, P], F32)
         make_identity(nc, ident_f32[:])
 
-        with tc.psum_pool(name="early", bufs=1) as early:
-            w_t = early.tile([P, HALVES, PACK, P], BF16)
+        with ExitStack() as first:
+            raw_pool = first.enter_context(tc.tile_pool(name="raw", bufs=1))
+            grouped_pool = first.enter_context(tc.tile_pool(name="grouped", bufs=4))
+            squares_pool = first.enter_context(tc.tile_pool(name="squares", bufs=4))
+            sums_pool = first.enter_context(tc.psum_pool(name="sums", bufs=1))
+
+            node_sums = [
+                sums_pool.tile([P, SUM_NODES], F32, name="node_sums%d" % h) for h in range(HALVES)
+            ]
+
+            raw = raw_pool.tile([P, GRAPHS, PACK, NODES], BF16)
+            for b, nodes in PIECES:
+                h1_b = h1[b].rearrange("(p j) n -> p j n", j=PACK)
+                nc.sync.dma_start(out=raw[:, b, :, nodes], in_=h1_b[:, :, nodes])
+
+            w_t = spare_pool.tile([P, HALVES, PACK, P], BF16, name="spare")
             for h in range(HALVES):
                 for j in range(PACK):
                     nc.tensor.transpose(w_t[:, h, j, :], w_rows[:, h, j::PACK], ident_bf16[:])
             w_grouped = keep.tile([P, HALVES, P, PACK], BF16, align_bytes=64)
             nc.scalar.copy(out=w_grouped[:], in_=w_t[:].rearrange("p h j o -> p h o j"))
 
-            gb_t = early.tile([P, P], BF16)
             gain_shift = keep.tile([P, 2 * HALVES], F32)
 
             def quantise_weights():
@@ -115,10 +121,6 @@ def tile_yuyipointupdate_pb_t_kernel(tc, h1, W2, g2, b2, out):
                     scales=w_scales[:],
                     in_=w_grouped[:].rearrange("p h o j -> p (h o j)"),
                 )
-
-            node_sums = [
-                early.tile([P, SUM_NODES], F32, name="node_sums%d" % h) for h in range(HALVES)
-            ]
 
             grouped_of = {}
 
@@ -142,18 +144,29 @@ def tile_yuyipointupdate_pb_t_kernel(tc, h1, W2, g2, b2, out):
                     in_=grouped_of[i][:, nodes, :].rearrange("p n j -> p (n j)"),
                 )
 
-            def multiply_for_statistics(i):
+            def multiply_for_squares(i):
                 b, nodes = PIECES[i]
                 for h in range(HALVES):
-                    z = z_pool.tile([P, NODES], F32)
+                    z = z_pool.tile([P, NODES], F32, name="z")
                     product(z[:, nodes], b, h, nodes, True, True)
                     z_of[i, h] = z
+
+            def multiply_for_sums(i):
+                b, nodes = PIECES[i]
                 for h in range(HALVES):
                     for n in range(nodes.start, nodes.stop, SUM_NODES):
                         product(
                             node_sums[h][:], b, h, slice(n, n + SUM_NODES),
                             b == 0 and n == 0, b == GRAPHS - 1 and n + SUM_NODES == NODES,
                         )
+
+            def multiply_for_statistics(i):
+                if i == len(PIECES) - 1:
+                    multiply_for_sums(i)
+                    multiply_for_squares(i)
+                else:
+                    multiply_for_squares(i)
+                    multiply_for_sums(i)
 
             def square_and_sum(i):
                 nodes = PIECES[i][1]
@@ -167,20 +180,29 @@ def tile_yuyipointupdate_pb_t_kernel(tc, h1, W2, g2, b2, out):
                     )
 
             for step in range(len(PIECES) + 2):
+                quantised_now = [
+                    i
+                    for i in (step - 1, step)
+                    if 0 <= i < len(PIECES) and step == (i if i == LAST_WHOLE else i + 1)
+                ]
                 if scalar_regroups(step + SCALAR_LEAD):
                     regroup(nc.scalar.copy, step + SCALAR_LEAD)
-                if 1 <= step <= 2:
-                    quantise(step - 1)
+                if step <= 2:
+                    for i in quantised_now:
+                        quantise(i)
                 if step < len(PIECES) and not scalar_regroups(step):
                     regroup(nc.vector.tensor_copy, step)
-                if 3 <= step <= len(PIECES):
-                    quantise(step - 1)
+                if step > 2:
+                    for i in quantised_now:
+                        quantise(i)
                 if step == 2:
                     quantise_weights()
                     multiply_for_statistics(0)
-                if 2 <= step <= len(PIECES):
-                    multiply_for_statistics(step - 1)
+                if step >= 2:
+                    for i in quantised_now:
+                        multiply_for_statistics(i)
                 if step == GAIN_STEP:
+                    gb_t = spare_pool.tile([P, P], BF16, name="spare")
                     nc.tensor.transpose(gb_t[:], gb_rows[:], ident_bf16[:])
                 if step == GAIN_STEP + 3:
                     nc.vector.tensor_copy(out=gain_shift[:], in_=gb_t[:, 0 : 2 * HALVES])
@@ -225,26 +247,45 @@ def tile_yuyipointupdate_pb_t_kernel(tc, h1, W2, g2, b2, out):
                 bias=gain_shift[:, HALVES + h : HALVES + h + 1],
             )
 
-        with tc.psum_pool(name="turned", bufs=4) as turned_pool:
+        with ExitStack() as second:
+            y_pool = second.enter_context(tc.tile_pool(name="y", bufs=4))
+            r_pool = second.enter_context(tc.tile_pool(name="r", bufs=3))
+            rows_pool = second.enter_context(tc.tile_pool(name="rows", bufs=12))
+            turned_pool = second.enter_context(tc.psum_pool(name="turned", bufs=2))
             y_of = {}
             r_of = {}
             banks_of = {}
 
+            def tile_groups(b):
+                size = 1 if b == GRAPHS - 1 else 2
+                return [range(t, t + size) for t in range(0, NODE_TILES, size)]
+
             def multiply(b):
                 for h in range(HALVES):
-                    z = z_pool.tile([P, NODES], F32)
-                    product(z[:], b, h, slice(0, NODES), True, True)
+                    if b == 0:
+                        z = spare_pool.tile([P, NODES], F32, name="spare")
+                    else:
+                        z = z_pool.tile([P, NODES], F32, name="z")
+                    product(z[:], b, h, WHOLE, True, True)
                     z_of[b, h] = z
+
+            def fetch(b):
+                y = y_pool.tile([P, HALVES, NODES], F32)
+                for h in range(HALVES):
+                    nc.vector.tensor_copy(out=y[:, h, :], in_=z_of[b, h][:])
+                y_of[b] = y
+
+            def normalise_fetched(b):
+                for h in range(HALVES):
+                    y = y_of[b][:, h, :]
+                    nc.vector.tensor_scalar(
+                        out=y, in0=y, scalar1=scale[:, h : h + 1], scalar2=shift[:, h : h + 1],
+                        op0=ALU.mult, op1=ALU.add,
+                    )
 
             def normalise(b):
                 y = y_pool.tile([P, HALVES, NODES], F32)
                 for h in range(HALVES):
-                    if (b, h) == (0, 1):
-                        nc.vector.tensor_scalar(
-                            out=y[:, h, :], in0=z_early[:], scalar1=scale[:, h : h + 1],
-                            scalar2=shift[:, h : h + 1], op0=ALU.mult, op1=ALU.add,
-                        )
-                        continue
                     nc.scalar.activation(
                         out=y[:, h, :],
                         in_=z_of[b, h][:],
@@ -257,25 +298,19 @@ def tile_yuyipointupdate_pb_t_kernel(tc, h1, W2, g2, b2, out):
             def leaky_relu(b):
                 r = r_pool.tile([P, HALVES, NODES], F32)
                 r_of[b] = r
-                if b == 0:
-                    parts = [(slice(1, 2), WHOLE), (slice(0, 1), WHOLE)]
-                elif b == GRAPHS - 1:
-                    parts = [(slice(0, HALVES), LEFT), (slice(0, HALVES), RIGHT)]
-                else:
-                    parts = [(slice(0, HALVES), WHOLE)]
-                for halves, nodes in parts:
-                    y = y_of[b][:, halves, nodes]
+                for nodes in (LEFT, RIGHT) if b in (0, GRAPHS - 1) else (WHOLE,):
+                    y = y_of[b][:, :, nodes]
                     nc.vector.scalar_tensor_tensor(
-                        out=r[:, halves, nodes], in0=y, scalar=NEG_SLOPE, in1=y,
+                        out=r[:, :, nodes], in0=y, scalar=NEG_SLOPE, in1=y,
                         op0=ALU.mult, op1=ALU.max,
                     )
 
             def turn(b):
                 banks = []
-                for pair in range(NODE_TILES // 2):
-                    turned = turned_pool.tile([P, 2, C_OUT], F32)
-                    for k in range(2):
-                        t = 2 * pair + k
+                for i, tiles in enumerate(tile_groups(b)):
+                    pool, name = ((turned_pool, "turned"), (spare_pool, "spare"), (z_pool, "z"))[min(i, 2)]
+                    turned = pool.tile([P, 2, C_OUT], F32, name=name)
+                    for k, t in enumerate(tiles):
                         for h in range(HALVES):
                             nc.tensor.transpose(
                                 turned[:, k, h * P : (h + 1) * P],
@@ -286,24 +321,35 @@ def tile_yuyipointupdate_pb_t_kernel(tc, h1, W2, g2, b2, out):
                 banks_of[b] = banks
 
             def empty_and_store(b):
+                engines = (nc.scalar.copy, nc.vector.tensor_copy)
+                if b == GRAPHS - 3:
+                    engines = (nc.scalar.copy, nc.scalar.copy)
                 out_tiles = out[b].rearrange("(t p) o -> p t o", p=P)
-                second = nc.scalar.copy if b == GRAPHS - 3 else nc.vector.tensor_copy
-                for pair, copy in enumerate((nc.scalar.copy, second)):
+                for i, tiles in enumerate(tile_groups(b)):
+                    copy = engines[i % 2]
                     rows = rows_pool.tile([P, 2, C_OUT], F32)
-                    copy(out=rows[:], in_=banks_of[b][pair][:])
-                    nc.sync.dma_start(out=out_tiles[:, 2 * pair : 2 * pair + 2, :], in_=rows[:])
+                    n = len(tiles)
+                    copy(out=rows[:, 0:n, :], in_=banks_of[b][i][:, 0:n, :])
+                    nc.sync.dma_start(
+                        out=out_tiles[:, tiles[0] : tiles[0] + n, :], in_=rows[:, 0:n, :]
+                    )
 
             multiply(0)
-            z_early = y_pool.tile([P, NODES], F32)
-            nc.vector.tensor_copy(out=z_early[:], in_=z_of[0, 1][:])
-            for step in range(GRAPHS + 2):
-                if step >= 2:
-                    turn(step - 2)
+            fetch(0)
+            multiply(1)
+            normalise_fetched(0)
+            for step in range(GRAPHS + 1):
+                if step >= 1:
+                    turn(step - 1)
+                if step + 2 < GRAPHS:
+                    multiply(step + 2)
+                if step == 0:
+                    for again in range(KEEP_CLOCK):
+                        idle = turned_pool.tile([P, 2, C_OUT], F32, name="turned")
+                        product(idle[:].rearrange("p k o -> p (k o)"), 0, 0, WHOLE, True, True)
                 if step + 1 < GRAPHS:
-                    multiply(step + 1)
+                    normalise(step + 1)
                 if step < GRAPHS:
-                    normalise(step)
-                if 1 <= step <= GRAPHS:
-                    leaky_relu(step - 1)
-                if step >= 2:
-                    empty_and_store(step - 2)
+                    leaky_relu(step)
+                if step >= 1:
+                    empty_and_store(step - 1)

@@ -22,6 +22,8 @@ HALVES = C_OUT // P
 NODE_TILES = NODES // P
 RUN = 4
 SCALAR_EVERY = 6
+SCALAR_FIRST = 2
+W_STEP = 3
 GAIN_STEP = 8
 SCALAR_LEAD = 2
 HALF_NODES = NODES // 2
@@ -32,7 +34,8 @@ PIECES = (
     + [(GRAPHS - 1, LEFT), (GRAPHS - 1, RIGHT)]
 )
 LAST_WHOLE = len(PIECES) - 3
-KEEP_CLOCK = 4
+KEEP_CLOCK = 7
+EARLY_STEP = 20
 EPS_BN = 1e-5
 NEG_SLOPE = 0.01
 SUM_NODES = 128
@@ -53,7 +56,8 @@ def tile_yuyipointupdate_pb_t_kernel(tc, h1, W2, g2, b2, out):
         w_scales = keep.tile([P, C_OUT], U8, align_bytes=64)
         h_codes = keep.tile([P, GRAPHS, NODES], U32, align_bytes=64)
         h_scales = keep.tile([P, GRAPHS, NODES], U8, align_bytes=64)
-        sum_sq_parts = keep.tile([P, HALVES, len(PIECES) + 2], F32)
+        z_early = keep.tile([P, HALVES, NODES], F32)
+        var_parts = keep.tile([P, HALVES, 2 + len(PIECES)], F32)
         z_of = {}
 
         def product(acc, b, h, n_cols, start, stop):
@@ -80,8 +84,7 @@ def tile_yuyipointupdate_pb_t_kernel(tc, h1, W2, g2, b2, out):
         one = keep.tile([P, 1], F32)
         nc.vector.memset(one[:], 1.0)
         nc.vector.tensor_scalar_mul(
-            out=sum_sq_parts[:, :, len(PIECES) + 1], in0=one[:].to_broadcast([P, HALVES]),
-            scalar1=EPS_BN * COUNT,
+            out=var_parts[:, :, 0], in0=one[:].to_broadcast([P, HALVES]), scalar1=EPS_BN
         )
         warm = keep.tile([P, 1], F32)
         nc.scalar.activation(out=warm[:], in_=one[:], func=ACT.Abs_reciprocal_sqrt)
@@ -93,7 +96,7 @@ def tile_yuyipointupdate_pb_t_kernel(tc, h1, W2, g2, b2, out):
 
         with ExitStack() as first:
             raw_pool = first.enter_context(tc.tile_pool(name="raw", bufs=1))
-            grouped_pool = first.enter_context(tc.tile_pool(name="grouped", bufs=4))
+            grouped_pool = first.enter_context(tc.tile_pool(name="grouped", bufs=6))
             squares_pool = first.enter_context(tc.tile_pool(name="squares", bufs=4))
             sums_pool = first.enter_context(tc.psum_pool(name="sums", bufs=1))
 
@@ -124,17 +127,26 @@ def tile_yuyipointupdate_pb_t_kernel(tc, h1, W2, g2, b2, out):
 
             grouped_of = {}
 
-            def scalar_regroups(i):
-                return i < len(PIECES) and PIECES[i][0] % SCALAR_EVERY == SCALAR_LEAD
-
-            def regroup(copy, i):
+            def scalar_nodes(i):
                 b, nodes = PIECES[i]
-                grouped = grouped_pool.tile([P, NODES, PACK], BF16, align_bytes=64)
+                if b % SCALAR_EVERY != SCALAR_FIRST:
+                    return None
+                return RIGHT if b + SCALAR_EVERY >= GRAPHS else nodes
+
+            def vector_nodes(i):
+                taken = scalar_nodes(i)
+                return PIECES[i][1] if taken is None else LEFT if taken == RIGHT else None
+
+            def regroup(copy, i, nodes):
+                if nodes is None:
+                    return
+                b = PIECES[i][0]
+                if i not in grouped_of:
+                    grouped_of[i] = grouped_pool.tile([P, NODES, PACK], BF16, align_bytes=64, name="grouped")
                 copy(
-                    out=grouped[:, nodes, :].rearrange("p (c i) j -> p c j i", i=RUN),
+                    out=grouped_of[i][:, nodes, :].rearrange("p (c i) j -> p c j i", i=RUN),
                     in_=raw[:, b, :, nodes].rearrange("p j (c i) -> p c j i", i=RUN),
                 )
-                grouped_of[i] = grouped
 
             def quantise(i):
                 b, nodes = PIECES[i]
@@ -176,7 +188,8 @@ def tile_yuyipointupdate_pb_t_kernel(tc, h1, W2, g2, b2, out):
                         out=squares[:, nodes],
                         in_=z_of[i, h][:, nodes],
                         func=ACT.Square,
-                        accum_out=sum_sq_parts[:, h, i : i + 1],
+                        scale=COUNT ** -0.5,
+                        accum_out=var_parts[:, h, 2 + i : 3 + i],
                     )
 
             for step in range(len(PIECES) + 2):
@@ -185,20 +198,20 @@ def tile_yuyipointupdate_pb_t_kernel(tc, h1, W2, g2, b2, out):
                     for i in (step - 1, step)
                     if 0 <= i < len(PIECES) and step == (i if i == LAST_WHOLE else i + 1)
                 ]
-                if scalar_regroups(step + SCALAR_LEAD):
-                    regroup(nc.scalar.copy, step + SCALAR_LEAD)
-                if step <= 2:
-                    for i in quantised_now:
-                        quantise(i)
-                if step < len(PIECES) and not scalar_regroups(step):
-                    regroup(nc.vector.tensor_copy, step)
-                if step > 2:
-                    for i in quantised_now:
-                        quantise(i)
-                if step == 2:
+                if step + SCALAR_LEAD < len(PIECES):
+                    i = step + SCALAR_LEAD
+                    regroup(nc.scalar.copy, i, scalar_nodes(i))
+                if step < len(PIECES):
+                    regroup(nc.vector.tensor_copy, step, vector_nodes(step))
+                for i in quantised_now:
+                    quantise(i)
+                if step == W_STEP:
                     quantise_weights()
-                    multiply_for_statistics(0)
-                if step >= 2:
+                    for i in range(W_STEP - 1):
+                        multiply_for_statistics(i)
+                    for i in range(W_STEP - 2):
+                        square_and_sum(i)
+                if step >= W_STEP:
                     for i in quantised_now:
                         multiply_for_statistics(i)
                 if step == GAIN_STEP:
@@ -206,36 +219,42 @@ def tile_yuyipointupdate_pb_t_kernel(tc, h1, W2, g2, b2, out):
                     nc.tensor.transpose(gb_t[:], gb_rows[:], ident_bf16[:])
                 if step == GAIN_STEP + 3:
                     nc.vector.tensor_copy(out=gain_shift[:], in_=gb_t[:, 0 : 2 * HALVES])
-                if step >= 2:
+                if step >= W_STEP:
                     square_and_sum(step - 2)
+                if step == EARLY_STEP:
+                    for h in range(HALVES):
+                        z = spare_pool.tile([P, NODES], F32, name="spare")
+                        product(z[:], 0, h, WHOLE, True, True)
+                        z_of[0, h] = z
+
+            for h in range(HALVES):
+                nc.vector.tensor_copy(out=z_early[:, h, :], in_=z_of[0, h][:])
 
             sum_z = keep.tile([P, HALVES], F32)
             for h in range(HALVES):
                 nc.vector.reduce_sum(out=sum_z[:, h : h + 1], in_=node_sums[h][:], axis=AXIS.X)
 
         nc.vector.scalar_tensor_tensor(
-            out=sum_sq_parts[:, :, len(PIECES)], in0=sum_z[:], scalar=-1.0 / COUNT, in1=sum_z[:],
+            out=var_parts[:, :, 1], in0=sum_z[:], scalar=-1.0 / COUNT ** 2, in1=sum_z[:],
             op0=ALU.mult, op1=ALU.mult,
+        )
+        most_of_var = keep.tile([P, HALVES], F32)
+        nc.vector.reduce_sum(
+            out=most_of_var[:], in_=var_parts[:, :, 0 : 1 + len(PIECES)], axis=AXIS.X
         )
         minus_gain_mean = keep.tile([P, HALVES], F32)
         nc.vector.scalar_tensor_tensor(
             out=minus_gain_mean[:], in0=sum_z[:], scalar=-1.0 / COUNT, in1=gain_shift[:, 0:HALVES],
             op0=ALU.mult, op1=ALU.mult,
         )
-        parts_copy = keep.tile([P, HALVES, len(PIECES) + 2], F32)
-        var_eps_sum = keep.tile([P, HALVES], F32)
         inv_std = keep.tile([P, HALVES], F32)
         scale = keep.tile([P, HALVES], F32)
         shift = keep.tile([P, HALVES], F32)
         for h in range(HALVES):
             nc.scalar.activation(
-                out=parts_copy[:, h, :], in_=sum_sq_parts[:, h, :], func=ACT.Identity,
-                accum_out=var_eps_sum[:, h : h + 1],
+                out=inv_std[:, h : h + 1], in_=var_parts[:, h, 1 + len(PIECES) :],
+                func=ACT.Abs_reciprocal_sqrt, bias=most_of_var[:, h : h + 1],
             )
-        nc.scalar.activation(
-            out=inv_std[:], in_=var_eps_sum[:], func=ACT.Abs_reciprocal_sqrt, scale=1.0 / COUNT
-        )
-
         for h in reversed(range(HALVES)):
             nc.scalar.activation(
                 out=scale[:, h : h + 1], in_=gain_shift[:, h : h + 1], func=ACT.Copy,
@@ -262,26 +281,20 @@ def tile_yuyipointupdate_pb_t_kernel(tc, h1, W2, g2, b2, out):
 
             def multiply(b):
                 for h in range(HALVES):
-                    if b == 0:
-                        z = spare_pool.tile([P, NODES], F32, name="spare")
-                    else:
-                        z = z_pool.tile([P, NODES], F32, name="z")
+                    z = z_pool.tile([P, NODES], F32, name="z")
                     product(z[:], b, h, WHOLE, True, True)
                     z_of[b, h] = z
 
-            def fetch(b):
+            def normalise_early():
                 y = y_pool.tile([P, HALVES, NODES], F32)
-                for h in range(HALVES):
-                    nc.vector.tensor_copy(out=y[:, h, :], in_=z_of[b, h][:])
-                y_of[b] = y
-
-            def normalise_fetched(b):
-                for h in range(HALVES):
-                    y = y_of[b][:, h, :]
-                    nc.vector.tensor_scalar(
-                        out=y, in0=y, scalar1=scale[:, h : h + 1], scalar2=shift[:, h : h + 1],
-                        op0=ALU.mult, op1=ALU.add,
-                    )
+                for nodes in (LEFT, RIGHT):
+                    for h in range(HALVES):
+                        nc.vector.tensor_scalar(
+                            out=y[:, h, nodes], in0=z_early[:, h, nodes],
+                            scalar1=scale[:, h : h + 1], scalar2=shift[:, h : h + 1],
+                            op0=ALU.mult, op1=ALU.add,
+                        )
+                y_of[0] = y
 
             def normalise(b):
                 y = y_pool.tile([P, HALVES, NODES], F32)
@@ -334,10 +347,8 @@ def tile_yuyipointupdate_pb_t_kernel(tc, h1, W2, g2, b2, out):
                         out=out_tiles[:, tiles[0] : tiles[0] + n, :], in_=rows[:, 0:n, :]
                     )
 
-            multiply(0)
-            fetch(0)
             multiply(1)
-            normalise_fetched(0)
+            normalise_early()
             for step in range(GRAPHS + 1):
                 if step >= 1:
                     turn(step - 1)

@@ -23,7 +23,7 @@ NODE_TILES = NODES // P
 RUN = 4
 SCALAR_EVERY = 6
 SCALAR_FIRST = 2
-W_STEP = 3
+W_STEP = 2
 GAIN_STEP = 8
 SCALAR_LEAD = 2
 HALF_NODES = NODES // 2
@@ -34,7 +34,7 @@ PIECES = (
     + [(GRAPHS - 1, LEFT), (GRAPHS - 1, RIGHT)]
 )
 LAST_WHOLE = len(PIECES) - 3
-KEEP_CLOCK = 7
+KEEP_CLOCK = 4
 EARLY_STEP = 20
 EPS_BN = 1e-5
 NEG_SLOPE = 0.01
@@ -129,13 +129,10 @@ def tile_yuyipointupdate_pb_t_kernel(tc, h1, W2, g2, b2, out):
 
             def scalar_nodes(i):
                 b, nodes = PIECES[i]
-                if b % SCALAR_EVERY != SCALAR_FIRST:
-                    return None
-                return RIGHT if b + SCALAR_EVERY >= GRAPHS else nodes
+                return nodes if b % SCALAR_EVERY == SCALAR_FIRST else None
 
             def vector_nodes(i):
-                taken = scalar_nodes(i)
-                return PIECES[i][1] if taken is None else LEFT if taken == RIGHT else None
+                return PIECES[i][1] if scalar_nodes(i) is None else None
 
             def regroup(copy, i, nodes):
                 if nodes is None:
@@ -201,10 +198,14 @@ def tile_yuyipointupdate_pb_t_kernel(tc, h1, W2, g2, b2, out):
                 if step + SCALAR_LEAD < len(PIECES):
                     i = step + SCALAR_LEAD
                     regroup(nc.scalar.copy, i, scalar_nodes(i))
+                if step <= W_STEP:
+                    for i in quantised_now:
+                        quantise(i)
                 if step < len(PIECES):
                     regroup(nc.vector.tensor_copy, step, vector_nodes(step))
-                for i in quantised_now:
-                    quantise(i)
+                if step > W_STEP:
+                    for i in quantised_now:
+                        quantise(i)
                 if step == W_STEP:
                     quantise_weights()
                     for i in range(W_STEP - 1):

@@ -36,6 +36,7 @@ PIECES = (
 LAST_WHOLE = len(PIECES) - 3
 KEEP_CLOCK = 4
 EARLY_STEP = 20
+DMA_ALIGN = 512
 EPS_BN = 1e-5
 NEG_SLOPE = 0.01
 SUM_NODES = 128
@@ -56,7 +57,7 @@ def tile_yuyipointupdate_pb_t_kernel(tc, h1, W2, g2, b2, out):
         w_scales = keep.tile([P, C_OUT], U8, align_bytes=64)
         h_codes = keep.tile([P, GRAPHS, NODES], U32, align_bytes=64)
         h_scales = keep.tile([P, GRAPHS, NODES], U8, align_bytes=64)
-        z_early = keep.tile([P, HALVES, NODES], F32)
+        z_early = keep.tile([P, HALVES, NODES], F32, align_bytes=DMA_ALIGN)
         var_parts = keep.tile([P, HALVES, 2 + len(PIECES)], F32)
         z_of = {}
 
@@ -104,7 +105,7 @@ def tile_yuyipointupdate_pb_t_kernel(tc, h1, W2, g2, b2, out):
                 sums_pool.tile([P, SUM_NODES], F32, name="node_sums%d" % h) for h in range(HALVES)
             ]
 
-            raw = raw_pool.tile([P, GRAPHS, PACK, NODES], BF16)
+            raw = raw_pool.tile([P, GRAPHS, PACK, NODES], BF16, align_bytes=DMA_ALIGN)
             for b, nodes in PIECES:
                 h1_b = h1[b].rearrange("(p j) n -> p j n", j=PACK)
                 nc.sync.dma_start(out=raw[:, b, :, nodes], in_=h1_b[:, :, nodes])
@@ -139,7 +140,7 @@ def tile_yuyipointupdate_pb_t_kernel(tc, h1, W2, g2, b2, out):
                     return
                 b = PIECES[i][0]
                 if i not in grouped_of:
-                    grouped_of[i] = grouped_pool.tile([P, NODES, PACK], BF16, align_bytes=64, name="grouped")
+                    grouped_of[i] = grouped_pool.tile([P, NODES, PACK], BF16, align_bytes=DMA_ALIGN, name="grouped")
                 copy(
                     out=grouped_of[i][:, nodes, :].rearrange("p (c i) j -> p c j i", i=RUN),
                     in_=raw[:, b, :, nodes].rearrange("p j (c i) -> p c j i", i=RUN),
@@ -287,7 +288,7 @@ def tile_yuyipointupdate_pb_t_kernel(tc, h1, W2, g2, b2, out):
                     z_of[b, h] = z
 
             def normalise_early():
-                y = y_pool.tile([P, HALVES, NODES], F32)
+                y = y_pool.tile([P, HALVES, NODES], F32, align_bytes=DMA_ALIGN)
                 for nodes in (LEFT, RIGHT):
                     for h in range(HALVES):
                         nc.vector.tensor_scalar(
@@ -298,7 +299,7 @@ def tile_yuyipointupdate_pb_t_kernel(tc, h1, W2, g2, b2, out):
                 y_of[0] = y
 
             def normalise(b):
-                y = y_pool.tile([P, HALVES, NODES], F32)
+                y = y_pool.tile([P, HALVES, NODES], F32, align_bytes=DMA_ALIGN)
                 for h in range(HALVES):
                     nc.scalar.activation(
                         out=y[:, h, :],
@@ -310,7 +311,7 @@ def tile_yuyipointupdate_pb_t_kernel(tc, h1, W2, g2, b2, out):
                 y_of[b] = y
 
             def leaky_relu(b):
-                r = r_pool.tile([P, HALVES, NODES], F32)
+                r = r_pool.tile([P, HALVES, NODES], F32, align_bytes=DMA_ALIGN)
                 r_of[b] = r
                 for nodes in (LEFT, RIGHT) if b in (0, GRAPHS - 1) else (WHOLE,):
                     y = y_of[b][:, :, nodes]
@@ -341,7 +342,7 @@ def tile_yuyipointupdate_pb_t_kernel(tc, h1, W2, g2, b2, out):
                 out_tiles = out[b].rearrange("(t p) o -> p t o", p=P)
                 for i, tiles in enumerate(tile_groups(b)):
                     copy = engines[i % 2]
-                    rows = rows_pool.tile([P, 2, C_OUT], F32)
+                    rows = rows_pool.tile([P, 2, C_OUT], F32, align_bytes=DMA_ALIGN)
                     n = len(tiles)
                     copy(out=rows[:, 0:n, :], in_=banks_of[b][i][:, 0:n, :])
                     nc.sync.dma_start(

from contextlib import ExitStack

import concourse.mybir as mybir
from concourse.masks import make_identity

BF16 = mybir.dt.bfloat16
F32 = mybir.dt.float32
U32 = mybir.dt.uint32
U8 = mybir.dt.uint8
FP8X4 = mybir.dt.float8_e4m3fn_x4
ACT = mybir.ActivationFunctionType
ALU = mybir.AluOpType
AXIS = mybir.AxisListType

P = 128
PACK = 4
GRAPHS = 24
C_IN = 512
NODES = 512
C_OUT = 256
HALVES = C_OUT // P
NODE_TILES = NODES // P
RUN = 4
SCALAR_EVERY = 6
SCALAR_FIRST = 2
W_STEP = 2
GAIN_STEP = 8
SCALAR_LEAD = 2
HALF_NODES = NODES // 2
LEFT, RIGHT, WHOLE = slice(0, HALF_NODES), slice(HALF_NODES, NODES), slice(0, NODES)
PIECES = (
    [(0, LEFT), (0, RIGHT)]
    + [(b, WHOLE) for b in range(1, GRAPHS - 1)]
    + [(GRAPHS - 1, LEFT), (GRAPHS - 1, RIGHT)]
)
LAST_WHOLE = len(PIECES) - 3
KEEP_CLOCK = 4
EARLY_STEP = 20
DMA_ALIGN = 512
EPS_BN = 1e-5
NEG_SLOPE = 0.01
SUM_NODES = 128
COUNT = GRAPHS * NODES

FLOPS = 2 * GRAPHS * C_OUT * C_IN * NODES


def tile_yuyipointupdate_pb_t_kernel(tc, h1, W2, g2, b2, out):
    nc = tc.nc
    with ExitStack() as ctx:
        ctx.enter_context(tc.manual_schedule())
        keep = ctx.enter_context(tc.tile_pool(name="keep", bufs=1))
        z_pool = ctx.enter_context(tc.psum_pool(name="z", bufs=2 * HALVES))
        spare_pool = ctx.enter_context(tc.psum_pool(name="spare", bufs=HALVES))

        w_codes = keep.tile([P, C_OUT], U32, align_bytes=64)
        w_scales = keep.tile([P, C_OUT], U8, align_bytes=64)
        h_codes = keep.tile([P, GRAPHS, NODES], U32, align_bytes=64)
        h_scales = keep.tile([P, GRAPHS, NODES], U8, align_bytes=64)
        z_early = keep.tile([P, HALVES, NODES], F32, align_bytes=DMA_ALIGN)
        var_parts = keep.tile([P, HALVES, 2 + len(PIECES)], F32)
        z_of = {}

        def product(acc, b, h, n_cols, start, stop):
            o_cols = slice(h * P, (h + 1) * P)
            nc.tensor.matmul_mx(
                out=acc,
                lhsT=w_codes[:, o_cols].bitcast(FP8X4),
                lhsT_scale=w_scales[:, o_cols],
                rhs=h_codes[:, b, n_cols].bitcast(FP8X4),
                rhs_scale=h_scales[:, b, n_cols],
                start=start,
                stop=stop,
            )

        w_rows = keep.tile([P, HALVES, C_IN], BF16)
        nc.scalar.dma_start(out=w_rows[:], in_=W2.rearrange("(h o) c -> o h c", h=HALVES))
        gb_rows = keep.tile([P, P], BF16)
        nc.vector.memset(gb_rows[:], 0.0)
        nc.scalar.dma_start(out=gb_rows[0:HALVES, :], in_=g2.rearrange("(h o) -> h o", h=HALVES))
        nc.scalar.dma_start(
            out=gb_rows[HALVES : 2 * HALVES, :], in_=b2.rearrange("(h o) -> h o", h=HALVES)
        )

        one = keep.tile([P, 1], F32)
        nc.vector.memset(one[:], 1.0)
        nc.vector.tensor_scalar_mul(
            out=var_parts[:, :, 0], in0=one[:].to_broadcast([P, HALVES]), scalar1=EPS_BN
        )
        warm = keep.tile([P, 1], F32)
        nc.scalar.activation(out=warm[:], in_=one[:], func=ACT.Abs_reciprocal_sqrt)

        ident_bf16 = keep.tile([P, P], BF16)
        make_identity(nc, ident_bf16[:])
        ident_f32 = keep.tile([P, P], F32)
        make_identity(nc, ident_f32[:])

        with ExitStack() as first:
            raw_pool = first.enter_context(tc.tile_pool(name="raw", bufs=1))
            grouped_pool = first.enter_context(tc.tile_pool(name="grouped", bufs=6))
            squares_pool = first.enter_context(tc.tile_pool(name="squares", bufs=4))
            sums_pool = first.enter_context(tc.psum_pool(name="sums", bufs=1))

            node_sums = [
                sums_pool.tile([P, SUM_NODES], F32, name="node_sums%d" % h) for h in range(HALVES)
            ]

            raw = raw_pool.tile([P, GRAPHS, PACK, NODES], BF16, align_bytes=DMA_ALIGN)
            for b, nodes in PIECES:
                h1_b = h1[b].rearrange("(p j) n -> p j n", j=PACK)
                nc.sync.dma_start(out=raw[:, b, :, nodes], in_=h1_b[:, :, nodes])

            w_t = spare_pool.tile([P, HALVES, PACK, P], BF16, name="spare")
            for h in range(HALVES):
                for j in range(PACK):
                    nc.tensor.transpose(w_t[:, h, j, :], w_rows[:, h, j::PACK], ident_bf16[:])
            w_grouped = keep.tile([P, HALVES, P, PACK], BF16, align_bytes=64)
            nc.scalar.copy(out=w_grouped[:], in_=w_t[:].rearrange("p h j o -> p h o j"))

            gain_shift = keep.tile([P, 2 * HALVES], F32)

            def quantise_weights():
                nc.vector.quantize_mx(
                    out=w_codes[:].bitcast(FP8X4),
                    scales=w_scales[:],
                    in_=w_grouped[:].rearrange("p h o j -> p (h o j)"),
                )

            grouped_of = {}

            def scalar_nodes(i):
                b, nodes = PIECES[i]
                return nodes if b % SCALAR_EVERY == SCALAR_FIRST else None

            def vector_nodes(i):
                return PIECES[i][1] if scalar_nodes(i) is None else None

            def regroup(copy, i, nodes):
                if nodes is None:
                    return
                b = PIECES[i][0]
                if i not in grouped_of:
                    grouped_of[i] = grouped_pool.tile([P, NODES, PACK], BF16, align_bytes=DMA_ALIGN, name="grouped")
                copy(
                    out=grouped_of[i][:, nodes, :].rearrange("p (c i) j -> p c j i", i=RUN),
                    in_=raw[:, b, :, nodes].rearrange("p j (c i) -> p c j i", i=RUN),
                )

            def quantise(i):
                b, nodes = PIECES[i]
                nc.vector.quantize_mx(
                    out=h_codes[:, b, nodes].bitcast(FP8X4),
                    scales=h_scales[:, b, nodes],
                    in_=grouped_of[i][:, nodes, :].rearrange("p n j -> p (n j)"),
                )

            def multiply_for_squares(i):
                b, nodes = PIECES[i]
                for h in range(HALVES):
                    z = z_pool.tile([P, NODES], F32, name="z")
                    product(z[:, nodes], b, h, nodes, True, True)
                    z_of[i, h] = z

            def multiply_for_sums(i):
                b, nodes = PIECES[i]
                for h in range(HALVES):
                    for n in range(nodes.start, nodes.stop, SUM_NODES):
                        product(
                            node_sums[h][:], b, h, slice(n, n + SUM_NODES),
                            b == 0 and n == 0, b == GRAPHS - 1 and n + SUM_NODES == NODES,
                        )

            def multiply_for_statistics(i):
                if i == len(PIECES) - 1:
                    multiply_for_sums(i)
                    multiply_for_squares(i)
                else:
                    multiply_for_squares(i)
                    multiply_for_sums(i)

            def square_and_sum(i):
                nodes = PIECES[i][1]
                for h in range(HALVES):
                    squares = squares_pool.tile([P, NODES], BF16)
                    nc.scalar.activation(
                        out=squares[:, nodes],
                        in_=z_of[i, h][:, nodes],
                        func=ACT.Square,
                        scale=COUNT ** -0.5,
                        accum_out=var_parts[:, h, 2 + i : 3 + i],
                    )

            for step in range(len(PIECES) + 2):
                quantised_now = [
                    i
                    for i in (step - 1, step)
                    if 0 <= i < len(PIECES) and step == (i if i == LAST_WHOLE else i + 1)
                ]
                if step + SCALAR_LEAD < len(PIECES):
                    i = step + SCALAR_LEAD
                    regroup(nc.scalar.copy, i, scalar_nodes(i))
                if step <= W_STEP:
                    for i in quantised_now:
                        quantise(i)
                if step < len(PIECES):
                    regroup(nc.vector.tensor_copy, step, vector_nodes(step))
                if step > W_STEP:
                    for i in quantised_now:
                        quantise(i)
                if step == W_STEP:
                    quantise_weights()
                    for i in range(W_STEP - 1):
                        multiply_for_statistics(i)
                    for i in range(W_STEP - 2):
                        square_and_sum(i)
                if step >= W_STEP:
                    for i in quantised_now:
                        multiply_for_statistics(i)
                if step == GAIN_STEP:
                    gb_t = spare_pool.tile([P, P], BF16, name="spare")
                    nc.tensor.transpose(gb_t[:], gb_rows[:], ident_bf16[:])
                if step == GAIN_STEP + 3:
                    nc.vector.tensor_copy(out=gain_shift[:], in_=gb_t[:, 0 : 2 * HALVES])
                if step >= W_STEP:
                    square_and_sum(step - 2)
                if step == EARLY_STEP:
                    for h in range(HALVES):
                        z = spare_pool.tile([P, NODES], F32, name="spare")
                        product(z[:], 0, h, WHOLE, True, True)
                        z_of[0, h] = z

            for h in range(HALVES):
                nc.vector.tensor_copy(out=z_early[:, h, :], in_=z_of[0, h][:])

            sum_z = keep.tile([P, HALVES], F32)
            for h in range(HALVES):
                nc.vector.reduce_sum(out=sum_z[:, h : h + 1], in_=node_sums[h][:], axis=AXIS.X)

        nc.vector.scalar_tensor_tensor(
            out=var_parts[:, :, 1], in0=sum_z[:], scalar=-1.0 / COUNT ** 2, in1=sum_z[:],
            op0=ALU.mult, op1=ALU.mult,
        )
        most_of_var = keep.tile([P, HALVES], F32)
        nc.vector.reduce_sum(
            out=most_of_var[:], in_=var_parts[:, :, 0 : 1 + len(PIECES)], axis=AXIS.X
        )
        minus_gain_mean = keep.tile([P, HALVES], F32)
        nc.vector.scalar_tensor_tensor(
            out=minus_gain_mean[:], in0=sum_z[:], scalar=-1.0 / COUNT, in1=gain_shift[:, 0:HALVES],
            op0=ALU.mult, op1=ALU.mult,
        )
        inv_std = keep.tile([P, HALVES], F32)
        scale = keep.tile([P, HALVES], F32)
        shift = keep.tile([P, HALVES], F32)
        for h in range(HALVES):
            nc.scalar.activation(
                out=inv_std[:, h : h + 1], in_=var_parts[:, h, 1 + len(PIECES) :],
                func=ACT.Abs_reciprocal_sqrt, bias=most_of_var[:, h : h + 1],
            )
        for h in reversed(range(HALVES)):
            nc.scalar.activation(
                out=scale[:, h : h + 1], in_=gain_shift[:, h : h + 1], func=ACT.Copy,
                scale=inv_std[:, h : h + 1],
            )
            nc.scalar.activation(
                out=shift[:, h : h + 1], in_=minus_gain_mean[:, h : h + 1], func=ACT.Identity,
                scale=inv_std[:, h : h + 1],
                bias=gain_shift[:, HALVES + h : HALVES + h + 1],
            )

        with ExitStack() as second:
            y_pool = second.enter_context(tc.tile_pool(name="y", bufs=4))
            r_pool = second.enter_context(tc.tile_pool(name="r", bufs=3))
            rows_pool = second.enter_context(tc.tile_pool(name="rows", bufs=12))
            turned_pool = second.enter_context(tc.psum_pool(name="turned", bufs=2))
            y_of = {}
            r_of = {}
            banks_of = {}

            def tile_groups(b):
                size = 1 if b == GRAPHS - 1 else 2
                return [range(t, t + size) for t in range(0, NODE_TILES, size)]

            def multiply(b):
                for h in range(HALVES):
                    z = z_pool.tile([P, NODES], F32, name="z")
                    product(z[:], b, h, WHOLE, True, True)
                    z_of[b, h] = z

            def normalise_early():
                y = y_pool.tile([P, HALVES, NODES], F32, align_bytes=DMA_ALIGN)
                for nodes in (LEFT, RIGHT):
                    for h in range(HALVES):
                        nc.vector.tensor_scalar(
                            out=y[:, h, nodes], in0=z_early[:, h, nodes],
                            scalar1=scale[:, h : h + 1], scalar2=shift[:, h : h + 1],
                            op0=ALU.mult, op1=ALU.add,
                        )
                y_of[0] = y

            def normalise(b):
                y = y_pool.tile([P, HALVES, NODES], F32, align_bytes=DMA_ALIGN)
                for h in range(HALVES):
                    nc.scalar.activation(
                        out=y[:, h, :],
                        in_=z_of[b, h][:],
                        func=ACT.Identity,
                        scale=scale[:, h : h + 1],
                        bias=shift[:, h : h + 1],
                    )
                y_of[b] = y

            def leaky_relu(b):
                r = r_pool.tile([P, HALVES, NODES], F32, align_bytes=DMA_ALIGN)
                r_of[b] = r
                for nodes in (LEFT, RIGHT) if b in (0, GRAPHS - 1) else (WHOLE,):
                    y = y_of[b][:, :, nodes]
                    nc.vector.scalar_tensor_tensor(
                        out=r[:, :, nodes], in0=y, scalar=NEG_SLOPE, in1=y,
                        op0=ALU.mult, op1=ALU.max,
                    )

            def turn(b):
                banks = []
                for i, tiles in enumerate(tile_groups(b)):
                    pool, name = ((turned_pool, "turned"), (spare_pool, "spare"), (z_pool, "z"))[min(i, 2)]
                    turned = pool.tile([P, 2, C_OUT], F32, name=name)
                    for k, t in enumerate(tiles):
                        for h in range(HALVES):
                            nc.tensor.transpose(
                                turned[:, k, h * P : (h + 1) * P],
                                r_of[b][:, h, t * P : (t + 1) * P],
                                ident_f32[:],
                            )
                    banks.append(turned)
                banks_of[b] = banks

            def empty_and_store(b):
                engines = (nc.scalar.copy, nc.vector.tensor_copy)
                if b == GRAPHS - 3:
                    engines = (nc.scalar.copy, nc.scalar.copy)
                out_tiles = out[b].rearrange("(t p) o -> p t o", p=P)
                for i, tiles in enumerate(tile_groups(b)):
                    copy = engines[i % 2]
                    rows = rows_pool.tile([P, 2, C_OUT], F32, align_bytes=DMA_ALIGN)
                    n = len(tiles)
                    copy(out=rows[:, 0:n, :], in_=banks_of[b][i][:, 0:n, :])
                    nc.sync.dma_start(
                        out=out_tiles[:, tiles[0] : tiles[0] + n, :], in_=rows[:, 0:n, :]
                    )

            multiply(1)
            normalise_early()
            for step in range(GRAPHS + 1):
                if step >= 1:
                    turn(step - 1)
                if step + 2 < GRAPHS:
                    multiply(step + 2)
                if step == 0:
                    for again in range(KEEP_CLOCK):
                        idle = turned_pool.tile([P, 2, C_OUT], F32, name="turned")
                        product(idle[:].rearrange("p k o -> p (k o)"), 0, 0, WHOLE, True, True)
                if step + 1 < GRAPHS:
                    normalise(step + 1)
                if step < GRAPHS:
                    leaky_relu(step)
                if step >= 1:
                    empty_and_store(step - 1)
